import numpy as np
import ml_dtypes


def mxq(x, axis, fmt="e4m3"):
    dtype, down = {"e4m3": (ml_dtypes.float8_e4m3fn, 7), "e5m2": (ml_dtypes.float8_e5m2, 14)}[fmt]
    v = np.moveaxis(np.asarray(x, np.float32).astype(ml_dtypes.bfloat16).astype(np.float64), axis, -1)
    blocks = v.reshape(v.shape[:-1] + (-1, 32))
    amax = np.abs(blocks).max(-1, keepdims=True)
    byte = np.maximum(np.where(amax > 0, np.frexp(amax)[1] - 1 + 127, 0) - down, 1)
    scale = np.exp2(byte - 127.0)
    codes = (blocks / scale).astype(np.float32).astype(dtype).astype(np.float64)
    return np.moveaxis((codes * scale).reshape(v.shape), -1, axis)


WIDE = False


def mx_kscale(k):
    if not WIDE:
        return np.ones(k)
    levels = np.array([10, -10, 5, -5, 0])
    if k % 512:
        return np.exp2(np.random.permutation(np.resize(levels, k // 32))).repeat(32)
    a = np.empty((k // 512, 16))
    for p in range(k // 512):
        a[p, :8] = np.random.permutation(np.resize(levels, 8))
        for g in range(8):
            far = levels[np.abs(levels - a[p, g]) >= 10]
            a[p, g + 8] = far[np.random.randint(len(far))]
    return np.exp2(a.ravel()).repeat(32)


BF16 = ml_dtypes.bfloat16


def bf(x):
    return np.asarray(x, np.float32).astype(BF16)


def f64(x):
    return np.asarray(x).astype(np.float64)


B, DI, DH = 4096, 1024, 128


def sigmoid(v):
    return 1.0 / (1.0 + np.exp(-v))


def setup_inputs():
    s = mx_kscale(DI)
    n = np.random.standard_normal
    a, c = 0.7 / np.sqrt(DI), 0.7 / np.sqrt(DH)
    keep = np.random.uniform(size=B) < 0.9
    return {
        "x": bf(n((B, DI)) * s),
        "h_minors": bf(n((B, DH))),
        "c_minors": bf(n((B, DH))),
        "s0": bf(n((B, DH))),
        "s1": bf(n((B, DH))),
        "s2": bf(n((B, DH))),
        "mask": bf(keep * (0.5 + 0.5 * np.random.uniform(size=B))),
        "weight_ih": bf(n((7 * DH, DI)) * a / s),
        "bias_ih": bf(n(7 * DH) * 0.3),
        "weight_hh": bf(n((4 * DH, DH)) * c),
        "bias_hh": bf(n(4 * DH) * 0.3),
        "weight_sh0": bf(n((DH, DH)) * c),
        "bias_sh0": bf(n(DH) * 0.3),
        "weight_sh1": bf(n((DH, DH)) * c),
        "bias_sh1": bf(n(DH) * 0.3),
        "weight_sh2": bf(n((DH, DH)) * c),
        "bias_sh2": bf(n(DH) * 0.3),
    }


def reference(x, h_minors, c_minors, s0, s1, s2, mask, weight_ih, bias_ih, weight_hh, bias_hh,
              weight_sh0, bias_sh0, weight_sh1, bias_sh1, weight_sh2, bias_sh2):
    d = DH
    m = f64(mask)[:, None]

    tmp = (mxq(f64(x), 1, "e4m3") @ mxq(f64(weight_ih), 1, "e4m3").T) + f64(bias_ih)
    tmp2 = f64(h_minors) @ f64(weight_hh).T + f64(bias_hh)
    tmp3 = np.concatenate([
        f64(s0) @ f64(weight_sh0).T + f64(bias_sh0),
        f64(s1) @ f64(weight_sh1).T + f64(bias_sh1),
        f64(s2) @ f64(weight_sh2).T + f64(bias_sh2),
    ], axis=1)

    tmp_in, tmp_s = tmp[:, :4 * d], tmp[:, 4 * d:]
    pre = tmp_in + tmp2
    ifo = sigmoid(pre[:, :3 * d])
    c_hat = pre[:, 3 * d:]
    i_g, f_g, o_g = ifo[:, :d], ifo[:, d:2 * d], ifo[:, 2 * d:]

    c_t = (f_g * f64(c_minors) + i_g * np.tanh(c_hat)) * m
    tc = np.tanh(c_t) * m
    h = o_g * tc

    bg = sigmoid(tmp_s + tmp3)
    b0, b1, b2 = bg[:, :d], bg[:, d:2 * d], bg[:, 2 * d:]

    s_0 = (b0 + 1.0 - o_g) * tc
    s_1 = (b1 + 2.0 - o_g - s_0) * 0.5 * tc
    s_2 = (b2 + 3.0 - o_g - (2.0 * s_0 + s_1)) * (1.0 / 3.0) * tc

    return (h, c_t, s_0, s_1, s_2)

@@ -1,0 +1,453 @@
+from contextlib import ExitStack
+
+import concourse.mybir as mybir
+from concourse.masks import make_identity
+
+F32 = mybir.dt.float32
+BF16 = mybir.dt.bfloat16
+U32 = mybir.dt.uint32
+U8 = mybir.dt.uint8
+FP8X4 = mybir.dt.float8_e4m3fn_x4
+ACT = mybir.ActivationFunctionType
+ALU = mybir.AluOpType
+
+P = 128
+B = 4096
+DI = 1024
+DH = 128
+N_GATES = 7
+I_G = 0
+F_G = 1
+O_G = 2
+C_HAT = 3
+B0_G = 4
+ROWS_PER_PARTITION = B // P
+TILES = 4
+BLOCK = TILES * P
+N_BLOCKS = B // BLOCK
+N_STEPS = N_BLOCKS * N_GATES
+PACK = 4
+PASSES = DI // (P * PACK)
+HALVES = 2
+CHUNK = PASSES * P
+N_SMALL = 5
+C_SLOT = 4
+W_AHEAD = 2
+
+FLOPS = 2 * B * N_GATES * DH * (DI + DH)
+
+
+def tile_share_lstm_cell_pa_t_kernel(
+    tc, x, h_minors, c_minors, s0, s1, s2, mask,
+    weight_ih, bias_ih, weight_hh, bias_hh,
+    weight_sh0, bias_sh0, weight_sh1, bias_sh1, weight_sh2, bias_sh2,
+    out_0, out_1, out_2, out_3, out_4,
+):
+    nc = tc.nc
+
+    x_rows = x.rearrange("(p j) k -> p j k", j=ROWS_PER_PARTITION)
+    small_rows = [
+        a.rearrange("(p j) d -> p j d", j=ROWS_PER_PARTITION)
+        for a in (h_minors, s0, s1, s2, c_minors)
+    ]
+    h_dram, c_dram, s0_dram, s1_dram, s2_dram = [
+        a.rearrange("(p j) d -> p j d", j=ROWS_PER_PARTITION)
+        for a in (out_0, out_1, out_2, out_3, out_4)
+    ]
+
+    with ExitStack() as stack:
+        stack.enter_context(tc.manual_schedule())
+        const = stack.enter_context(tc.tile_pool(name="const", bufs=1))
+        x_pool = stack.enter_context(tc.tile_pool(name="x_pool", bufs=3))
+        small_pool = stack.enter_context(tc.tile_pool(name="small_pool", bufs=4))
+        operand_pool = stack.enter_context(tc.tile_pool(name="operand_pool", bufs=2))
+        pre_pool = stack.enter_context(tc.tile_pool(name="pre_pool", bufs=4))
+        gate_pool = stack.enter_context(tc.tile_pool(name="gate_pool", bufs=2))
+        finish_pool = stack.enter_context(tc.tile_pool(name="finish_pool", bufs=2))
+        out_pool = stack.enter_context(tc.tile_pool(name="out_pool", bufs=2))
+        psum_in = stack.enter_context(tc.psum_pool(name="psum_in", bufs=2))
+        psum_plain = stack.enter_context(tc.psum_pool(name="psum_plain", bufs=2))
+        psum_mx = stack.enter_context(tc.psum_pool(name="psum_mx", bufs=2))
+        psum_back = stack.enter_context(tc.psum_pool(name="psum_back", bufs=2))
+
+        held = {}
+
+        def live(k):
+            return 0 <= k < N_BLOCKS
+
+        def block_rows(k):
+            return slice(k * TILES, (k + 1) * TILES)
+
+        def load_x(k, first, count):
+            if not live(k):
+                return
+            if first == 0:
+                x_sb = x_pool.tile([P, TILES * DI], BF16, name="x_sb")
+                held["x_tiles", k] = x_sb[:].rearrange("p (t k) -> p t k", t=TILES)
+                held["x_words", k] = x_sb[:].bitcast(F32).rearrange("p (t w) -> p t w", t=TILES)
+            nc.sync.dma_start(
+                out=held["x_tiles", k][:, first:first + count, :],
+                in_=x_rows[:, k * TILES + first:k * TILES + first + count, :],
+            )
+
+        def load_small(k):
+            if not live(k):
+                return
+            small_sb = small_pool.tile([P, N_SMALL * TILES * DH], BF16, name="small_sb")
+            small = small_sb[:].rearrange("p (a t d) -> p a t d", a=N_SMALL, t=TILES)
+            for a in range(N_SMALL):
+                nc.sync.dma_start(out=small[:, a], in_=small_rows[a][:, block_rows(k), :])
+            held["small", k] = small
+
+        w_sb = const.tile([P, N_GATES * DI], BF16, name="w_sb")
+        w_words = w_sb[:].bitcast(F32).rearrange("p (c w) -> p c w", c=N_GATES)
+
+        def load_weights(c):
+            nc.sync.dma_start(out=w_sb[:, c * DI:(c + 1) * DI], in_=weight_ih[c * P:(c + 1) * P, :])
+
+        def turn_words(words, pool, tag):
+            turned = pool.tile([P, PASSES, HALVES, P], F32, name="turned", tag=tag)
+            for g in range(PASSES):
+                for u in range(HALVES):
+                    pass_words = words[:, g * HALVES * P + u:(g + 1) * HALVES * P:HALVES]
+                    nc.tensor.transpose(turned[:, g, u, :], pass_words, ident_f32[:])
+            return turned[:].rearrange("q g u r -> q g r u")
+
+        def turn_x(k, t):
+            if live(k):
+                held["x_ps", k, t] = turn_words(held["x_words", k][:, t, :], psum_in, "in")
+
+        def copy_x(k, t, copy_out):
+            if not live(k):
+                return
+            if t == 0:
+                grouped = operand_pool.tile([P, PASSES * BLOCK * PACK], BF16, name="grouped", align_bytes=64)
+                held["grouped", k] = grouped
+            grouped_words = held["grouped", k][:].bitcast(F32).rearrange(
+                "q (g r u) -> q g r u", g=PASSES, u=HALVES
+            )
+            copy_out(out=grouped_words[:, :, t * P:(t + 1) * P, :], in_=held["x_ps", k, t])
+
+        def quantise_x(k):
+            if not live(k):
+                return
+            x_codes = operand_pool.tile([P, PASSES * BLOCK], U32, name="x_codes", align_bytes=64)
+            x_scales = operand_pool.tile([P, PASSES * BLOCK], U8, name="x_scales", align_bytes=64)
+            nc.vector.quantize_mx(
+                out=x_codes[:].bitcast(FP8X4), scales=x_scales[:], in_=held["grouped", k][:]
+            )
+            held["x_codes", k] = x_codes
+            held["x_scales", k] = x_scales
+
+        def turn_pair(k, pair):
+            if not live(k):
+                return
+            pair_ps = psum_in.tile([P, 2, TILES, P], BF16, name="pair_ps", tag="in")
+            for i in range(2):
+                for t in range(TILES):
+                    nc.tensor.transpose(
+                        pair_ps[:, i, t, :], held["small", k][:, 2 * pair + i, t, :], ident_bf16[:]
+                    )
+            held["pair_ps", k, pair] = pair_ps
+
+        def copy_pair(k, pair):
+            if not live(k):
+                return
+            if pair == 0:
+                turned_small = operand_pool.tile([P, (N_SMALL - 1) * BLOCK], BF16, name="turned_small")
+                held["turned_small", k] = turned_small[:].rearrange(
+                    "d (a r) -> d a r", a=N_SMALL - 1
+                )
+            nc.scalar.copy(
+                out=held["turned_small", k][:, 2 * pair:2 * pair + 2, :],
+                in_=held["pair_ps", k, pair][:].rearrange("d a t r -> d a (t r)"),
+            )
+
+        w_grouped = const.tile([P, N_GATES * CHUNK * PACK], BF16, name="w_grouped", align_bytes=64)
+        w_grouped_words = w_grouped[:].bitcast(F32).rearrange(
+            "q (c g r u) -> q c g r u", c=N_GATES, g=PASSES, u=HALVES
+        )
+        w_codes = const.tile([P, N_GATES * CHUNK], U32, name="w_codes", align_bytes=64)
+        w_scales = const.tile([P, N_GATES * CHUNK], U8, name="w_scales", align_bytes=64)
+
+        def prepare_weights(c):
+            copy_out = nc.scalar.copy if c % 2 == 0 else nc.vector.tensor_copy
+            copy_out(out=w_grouped_words[:, c], in_=turn_words(w_words[:, c, :], psum_back, "back"))
+            nc.vector.quantize_mx(
+                out=w_codes[:, c * CHUNK:(c + 1) * CHUNK].bitcast(FP8X4),
+                scales=w_scales[:, c * CHUNK:(c + 1) * CHUNK],
+                in_=w_grouped[:, c * CHUNK * PACK:(c + 1) * CHUNK * PACK],
+            )
+
+        def gate_matmuls(n):
+            if not 0 <= n < N_STEPS:
+                return
+            k, j = divmod(n, N_GATES)
+            plain = psum_plain.tile([P, BLOCK], F32, name="plain")
+            nc.tensor.matmul(
+                plain[:], lhsT=small_wT[:, j, :], rhs=held["turned_small", k][:, max(0, j - C_HAT), :],
+                start=True, stop=True,
+            )
+            acc = psum_mx.tile([P, BLOCK], F32, name="acc")
+            for g in range(PASSES):
+                w_cols = slice(j * CHUNK + g * P, j * CHUNK + (g + 1) * P)
+                x_cols = slice(g * BLOCK, (g + 1) * BLOCK)
+                nc.tensor.matmul_mx(
+                    out=acc[:],
+                    lhsT=w_codes[:, w_cols].bitcast(FP8X4),
+                    lhsT_scale=w_scales[:, w_cols],
+                    rhs=held["x_codes", k][:, x_cols].bitcast(FP8X4),
+                    rhs_scale=held["x_scales", k][:, x_cols],
+                    start=(g == 0),
+                    stop=(g == PASSES - 1),
+                )
+            held["plain", n] = plain
+            held["acc", n] = acc
+
+        def gate_sum(n):
+            if not 0 <= n < N_STEPS:
+                return
+            pre = pre_pool.tile([P, BLOCK], F32, name="pre")
+            nc.scalar.copy(out=pre[:], in_=held["plain", n][:])
+            nc.vector.tensor_tensor(out=pre[:], in0=held["acc", n][:], in1=pre[:], op=ALU.add)
+            held["pre", n] = pre
+
+        def gate_function(n):
+            if not 0 <= n < N_STEPS:
+                return
+            k, j = divmod(n, N_GATES)
+            if j == 0:
+                held["gate", k] = gate_pool.tile([P, N_GATES, BLOCK], F32, name="gate")
+            if j == B0_G:
+                held["b_less_o", k] = gate_pool.tile([P, 3, BLOCK], F32, name="b_less_o")
+            gate = held["gate", k]
+            nc.scalar.activation(
+                out=gate[:, j, :], in_=held["pre", n][:], func=ACT.Tanh if j == C_HAT else ACT.Sigmoid,
+                bias=bias[:, j:j + 1],
+            )
+            if j == C_HAT:
+                i_tanh = gate_pool.tile([P, BLOCK], F32, name="i_tanh")
+                nc.gpsimd.tensor_tensor(out=i_tanh[:], in0=gate[:, I_G, :], in1=gate[:, C_HAT, :], op=ALU.mult)
+                held["i_tanh", k] = i_tanh
+            if j >= B0_G:
+                nc.gpsimd.tensor_tensor(
+                    out=held["b_less_o", k][:, j - B0_G, :], in0=gate[:, j, :], in1=gate[:, O_G, :],
+                    op=ALU.subtract,
+                )
+
+        def gate_step(k, j):
+            n = k * N_GATES + j
+            if n + W_AHEAD < N_GATES:
+                prepare_weights(n + W_AHEAD)
+            gate_matmuls(n)
+            gate_sum(n - 1)
+            gate_function(n - 2)
+
+        def turn_back(k, name, features):
+            rows_ps = psum_back.tile([P, TILES, DH], F32, name="rows_ps", tag="back")
+            for t in range(TILES):
+                nc.tensor.transpose(rows_ps[:, t, :], features[:, t * P:(t + 1) * P], ident_f32[:])
+            held[name, k] = rows_ps
+
+        def turn_back_cell(k):
+            if live(k):
+                turn_back(k, "f_rows", held["gate", k][:, F_G, :])
+                turn_back(k, "i_tanh_rows", held["i_tanh", k][:])
+
+        def turn_back_first(k):
+            if live(k):
+                turn_back(k, "o_rows", held["gate", k][:, O_G, :])
+                turn_back(k, "g0_rows", held["b_less_o", k][:, 0, :])
+
+        def turn_back_last(k):
+            if live(k):
+                turn_back(k, "g1_rows", held["b_less_o", k][:, 1, :])
+                turn_back(k, "g2_rows", held["b_less_o", k][:, 2, :])
+
+        def new_rows(pool, name, k):
+            held[name, k] = pool.tile([P, TILES, DH], F32, name=name)
+            return held[name, k]
+
+        def mask_of(k, t):
+            return m[:, k * TILES + t:k * TILES + t + 1]
+
+        def store(dram, k, name):
+            nc.sync.dma_start(out=dram[:, block_rows(k), :], in_=held[name, k][:])
+
+        def cell_product(k):
+            if live(k):
+                f_c = new_rows(finish_pool, "f_c", k)
+                for t in range(TILES):
+                    nc.vector.scalar_tensor_tensor(
+                        out=f_c[:, t, :], in0=held["f_rows", k][:, t, :], scalar=mask_of(k, t),
+                        in1=held["small", k][:, C_SLOT, t, :], op0=ALU.mult, op1=ALU.mult,
+                    )
+
+        def cell_state(k):
+            if live(k):
+                c_out = new_rows(out_pool, "c_out", k)
+                for t in range(TILES):
+                    nc.vector.scalar_tensor_tensor(
+                        out=c_out[:, t, :], in0=held["i_tanh_rows", k][:, t, :], scalar=mask_of(k, t),
+                        in1=held["f_c", k][:, t, :], op0=ALU.mult, op1=ALU.add,
+                    )
+
+        def cell_tanh(k):
+            if live(k):
+                tanh_c = new_rows(finish_pool, "tanh_c", k)
+                nc.scalar.activation(out=tanh_c[:], in_=held["c_out", k][:], func=ACT.Tanh)
+                tc_rows = new_rows(finish_pool, "tc_rows", k)
+                for t in range(TILES):
+                    nc.scalar.activation(
+                        out=tc_rows[:, t, :], in_=tanh_c[:, t, :], func=ACT.Copy, scale=mask_of(k, t)
+                    )
+
+        def output_h(k):
+            if live(k):
+                nc.vector.tensor_tensor(
+                    out=new_rows(out_pool, "h_out", k)[:], in0=held["o_rows", k][:], in1=held["tc_rows", k][:],
+                    op=ALU.mult,
+                )
+
+        def output_s0(k):
+            if live(k):
+                nc.vector.scalar_tensor_tensor(
+                    out=new_rows(out_pool, "s0_out", k)[:], in0=held["g0_rows", k][:], scalar=1.0,
+                    in1=held["tc_rows", k][:], op0=ALU.add, op1=ALU.mult,
+                )
+                store(h_dram, k, "h_out")
+                store(c_dram, k, "c_out")
+                store(s0_dram, k, "s0_out")
+
+        def sums_s1_s2(k):
+            if live(k):
+                nc.vector.scalar_tensor_tensor(
+                    out=new_rows(finish_pool, "s1_sum", k)[:], in0=held["g1_rows", k][:], scalar=2.0,
+                    in1=held["s0_out", k][:], op0=ALU.add, op1=ALU.subtract,
+                )
+                nc.vector.scalar_tensor_tensor(
+                    out=new_rows(finish_pool, "s2_part", k)[:], in0=held["s0_out", k][:], scalar=-2.0,
+                    in1=held["g2_rows", k][:], op0=ALU.mult, op1=ALU.add,
+                )
+
+        def output_s1(k):
+            if live(k):
+                nc.vector.scalar_tensor_tensor(
+                    out=new_rows(out_pool, "s1_out", k)[:], in0=held["s1_sum", k][:], scalar=0.5,
+                    in1=held["tc_rows", k][:], op0=ALU.mult, op1=ALU.mult,
+                )
+                nc.vector.scalar_tensor_tensor(
+                    out=new_rows(finish_pool, "s2_sum", k)[:], in0=held["s2_part", k][:], scalar=3.0,
+                    in1=held["s1_out", k][:], op0=ALU.add, op1=ALU.subtract,
+                )
+
+        def output_s2(k):
+            if live(k):
+                nc.vector.scalar_tensor_tensor(
+                    out=new_rows(out_pool, "s2_out", k)[:], in0=held["s2_sum", k][:], scalar=1.0 / 3.0,
+                    in1=held["tc_rows", k][:], op0=ALU.mult, op1=ALU.mult,
+                )
+                store(s1_dram, k, "s1_out")
+                store(s2_dram, k, "s2_out")
+
+        ident_f32 = const.tile([P, P], F32, name="ident_f32")
+        make_identity(nc, ident_f32[:])
+        ident_bf16 = const.tile([P, P], BF16, name="ident_bf16")
+        make_identity(nc, ident_bf16[:])
+
+        small_w = const.tile([P, N_GATES, DH], BF16, name="small_w")
+        nc.scalar.dma_start(
+            out=small_w[:, 0:B0_G, :], in_=weight_hh.rearrange("(c p) d -> p c d", p=P)
+        )
+        for i, w in enumerate((weight_sh0, weight_sh1, weight_sh2)):
+            nc.scalar.dma_start(out=small_w[:, B0_G + i, :], in_=w)
+
+        for t in range(TILES):
+            load_x(0, t, 1)
+        load_weights(0)
+        load_weights(1)
+        load_small(0)
+        bias_rows = const.tile([P, P], BF16, name="bias_rows")
+        nc.vector.memset(bias_rows[:], 0.0)
+        nc.sync.dma_start(out=bias_rows[0:N_GATES, :], in_=bias_ih.rearrange("(r d) -> r d", d=DH))
+        nc.sync.dma_start(
+            out=bias_rows[N_GATES:N_GATES + B0_G, :], in_=bias_hh.rearrange("(r d) -> r d", d=DH)
+        )
+        for i, b in enumerate((bias_sh0, bias_sh1, bias_sh2)):
+            row = N_GATES + B0_G + i
+            nc.sync.dma_start(out=bias_rows[row:row + 1, :], in_=b.rearrange("(r d) -> r d", d=DH))
+        load_x(1, 0, 2)
+        load_weights(2)
+        load_weights(3)
+        load_x(1, 2, 2)
+        load_weights(4)
+        load_weights(5)
+        load_weights(6)
+        load_small(1)
+        mask_bf16 = const.tile([P, ROWS_PER_PARTITION], BF16, name="mask_bf16")
+        nc.sync.dma_start(out=mask_bf16[:], in_=mask.rearrange("(p j) -> p j", j=ROWS_PER_PARTITION))
+
+        small_ps = psum_in.tile([P, N_GATES, P], BF16, name="small_ps", tag="in")
+        for c in range(N_GATES):
+            nc.tensor.transpose(small_ps[:, c, :], small_w[:, c, :], ident_bf16[:])
+        small_wT = const.tile([P, N_GATES, DH], BF16, name="small_wT")
+        nc.vector.tensor_copy(out=small_wT[:], in_=small_ps[:])
+
+        for t in range(TILES):
+            turn_x(0, t)
+            copy_x(0, t, nc.scalar.copy if t % 2 == 0 else nc.vector.tensor_copy)
+        quantise_x(0)
+        for c in range(W_AHEAD):
+            prepare_weights(c)
+        for pair in range(2):
+            turn_pair(0, pair)
+            copy_pair(0, pair)
+
+        bias_ps = psum_in.tile([P, P], BF16, name="bias_ps", tag="in")
+        nc.tensor.transpose(bias_ps[:], bias_rows[:], ident_bf16[:])
+        bias_cols = const.tile([P, 2 * N_GATES], F32, name="bias_cols")
+        nc.vector.tensor_copy(out=bias_cols[:], in_=bias_ps[:, 0:2 * N_GATES])
+        bias = const.tile([P, N_GATES], F32, name="bias")
+        nc.vector.tensor_tensor(
+            out=bias[:], in0=bias_cols[:, 0:N_GATES], in1=bias_cols[:, N_GATES:2 * N_GATES], op=ALU.add
+        )
+        m = const.tile([P, ROWS_PER_PARTITION], F32, name="m")
+        nc.gpsimd.tensor_copy(out=m[:], in_=mask_bf16[:])
+
+        for k in range(N_BLOCKS + 2):
+            load_x(k + 2, 0, TILES)
+            load_small(k + 2)
+
+            turn_x(k + 1, 0)
+            turn_x(k + 1, 1)
+            turn_back_cell(k - 1)
+            gate_step(k, 0)
+            copy_x(k + 1, 0, nc.scalar.copy)
+            cell_product(k - 1)
+            copy_x(k + 1, 1, nc.vector.tensor_copy)
+            gate_step(k, 1)
+            cell_state(k - 1)
+
+            turn_x(k + 1, 2)
+            turn_x(k + 1, 3)
+            turn_back_last(k - 2)
+            gate_step(k, 2)
+            copy_x(k + 1, 2, nc.scalar.copy)
+            sums_s1_s2(k - 2)
+            copy_x(k + 1, 3, nc.vector.tensor_copy)
+            gate_step(k, 3)
+            output_s1(k - 2)
+            gate_step(k, 4)
+            cell_tanh(k - 1)
+            output_s2(k - 2)
+            quantise_x(k + 1)
+
+            turn_pair(k + 1, 0)
+            turn_pair(k + 1, 1)
+            turn_back_first(k - 1)
+            gate_step(k, 5)
+            copy_pair(k + 1, 0)
+            output_h(k - 1)
+            gate_step(k, 6)
+            copy_pair(k + 1, 1)
+            output_s0(k - 1)

@@ -361,6 +361,9 @@ def tile_share_lstm_cell_pa_t_kernel(
         )
         for i, w in enumerate((weight_sh0, weight_sh1, weight_sh2)):
             nc.scalar.dma_start(out=small_w[:, B0_G + i, :], in_=w)
+        warm = const.tile([P, 1], F32, name="warm")
+        nc.vector.memset(warm[:], 0.0)
+        nc.scalar.activation(out=warm[:], in_=warm[:], func=ACT.Sigmoid)
 
         for t in range(TILES):
             load_x(0, t, 1)
@@ -369,13 +372,13 @@ def tile_share_lstm_cell_pa_t_kernel(
         load_small(0)
         bias_rows = const.tile([P, P], BF16, name="bias_rows")
         nc.vector.memset(bias_rows[:], 0.0)
-        nc.sync.dma_start(out=bias_rows[0:N_GATES, :], in_=bias_ih.rearrange("(r d) -> r d", d=DH))
-        nc.sync.dma_start(
+        nc.gpsimd.dma_start(out=bias_rows[0:N_GATES, :], in_=bias_ih.rearrange("(r d) -> r d", d=DH))
+        nc.gpsimd.dma_start(
             out=bias_rows[N_GATES:N_GATES + B0_G, :], in_=bias_hh.rearrange("(r d) -> r d", d=DH)
         )
         for i, b in enumerate((bias_sh0, bias_sh1, bias_sh2)):
             row = N_GATES + B0_G + i
-            nc.sync.dma_start(out=bias_rows[row:row + 1, :], in_=b.rearrange("(r d) -> r d", d=DH))
+            nc.gpsimd.dma_start(out=bias_rows[row:row + 1, :], in_=b.rearrange("(r d) -> r d", d=DH))
         load_x(1, 0, 2)
         load_weights(2)
         load_weights(3)
@@ -385,7 +388,7 @@ def tile_share_lstm_cell_pa_t_kernel(
         load_weights(6)
         load_small(1)
         mask_bf16 = const.tile([P, ROWS_PER_PARTITION], BF16, name="mask_bf16")
-        nc.sync.dma_start(out=mask_bf16[:], in_=mask.rearrange("(p j) -> p j", j=ROWS_PER_PARTITION))
+        nc.gpsimd.dma_start(out=mask_bf16[:], in_=mask.rearrange("(p j) -> p j", j=ROWS_PER_PARTITION))
 
         small_ps = psum_in.tile([P, N_GATES, P], BF16, name="small_ps", tag="in")
         for c in range(N_GATES):

@@ -65,10 +65,10 @@ def tile_share_lstm_cell_pa_t_kernel(
         gate_pool = stack.enter_context(tc.tile_pool(name="gate_pool", bufs=2))
         finish_pool = stack.enter_context(tc.tile_pool(name="finish_pool", bufs=2))
         out_pool = stack.enter_context(tc.tile_pool(name="out_pool", bufs=2))
-        psum_in = stack.enter_context(tc.psum_pool(name="psum_in", bufs=2))
+        psum_in = stack.enter_context(tc.psum_pool(name="psum_in", bufs=3))
         psum_plain = stack.enter_context(tc.psum_pool(name="psum_plain", bufs=2))
-        psum_mx = stack.enter_context(tc.psum_pool(name="psum_mx", bufs=2))
-        psum_back = stack.enter_context(tc.psum_pool(name="psum_back", bufs=2))
+        psum_mx = stack.enter_context(tc.psum_pool(name="psum_mx", bufs=3))
+        psum_back = psum_in
 
         held = {}
 
@@ -172,7 +172,7 @@ def tile_share_lstm_cell_pa_t_kernel(
 
         def prepare_weights(c):
             copy_out = nc.scalar.copy if c % 2 == 0 else nc.vector.tensor_copy
-            copy_out(out=w_grouped_words[:, c], in_=turn_words(w_words[:, c, :], psum_back, "back"))
+            copy_out(out=w_grouped_words[:, c], in_=turn_words(w_words[:, c, :], psum_back, "in"))
             nc.vector.quantize_mx(
                 out=w_codes[:, c * CHUNK:(c + 1) * CHUNK].bitcast(FP8X4),
                 scales=w_scales[:, c * CHUNK:(c + 1) * CHUNK],
@@ -244,25 +244,17 @@ def tile_share_lstm_cell_pa_t_kernel(
             gate_function(n - 2)
 
         def turn_back(k, name, features):
-            rows_ps = psum_back.tile([P, TILES, DH], F32, name="rows_ps", tag="back")
+            rows_ps = psum_back.tile([P, TILES, DH], F32, name="rows_ps", tag="in")
             for t in range(TILES):
                 nc.tensor.transpose(rows_ps[:, t, :], features[:, t * P:(t + 1) * P], ident_f32[:])
             held[name, k] = rows_ps
 
-        def turn_back_cell(k):
+        def tb(k, name):
             if live(k):
-                turn_back(k, "f_rows", held["gate", k][:, F_G, :])
-                turn_back(k, "i_tanh_rows", held["i_tanh", k][:])
-
-        def turn_back_first(k):
-            if live(k):
-                turn_back(k, "o_rows", held["gate", k][:, O_G, :])
-                turn_back(k, "g0_rows", held["b_less_o", k][:, 0, :])
-
-        def turn_back_last(k):
-            if live(k):
-                turn_back(k, "g1_rows", held["b_less_o", k][:, 1, :])
-                turn_back(k, "g2_rows", held["b_less_o", k][:, 2, :])
+                if name == "f_rows": turn_back(k, name, held["gate", k][:, F_G, :])
+                elif name == "o_rows": turn_back(k, name, held["gate", k][:, O_G, :])
+                elif name == "i_tanh_rows": turn_back(k, name, held["i_tanh", k][:])
+                else: turn_back(k, name, held["b_less_o", k][:, int(name[1]), :])
 
         def new_rows(pool, name, k):
             held[name, k] = pool.tile([P, TILES, DH], F32, name=name)
@@ -319,12 +311,15 @@ def tile_share_lstm_cell_pa_t_kernel(
                 store(c_dram, k, "c_out")
                 store(s0_dram, k, "s0_out")
 
-        def sums_s1_s2(k):
+        def sums1(k):
             if live(k):
                 nc.vector.scalar_tensor_tensor(
                     out=new_rows(finish_pool, "s1_sum", k)[:], in0=held["g1_rows", k][:], scalar=2.0,
                     in1=held["s0_out", k][:], op0=ALU.add, op1=ALU.subtract,
                 )
+
+        def sums2(k):
+            if live(k):
                 nc.vector.scalar_tensor_tensor(
                     out=new_rows(finish_pool, "s2_part", k)[:], in0=held["s0_out", k][:], scalar=-2.0,
                     in1=held["g2_rows", k][:], op0=ALU.mult, op1=ALU.add,
@@ -418,39 +413,39 @@ def tile_share_lstm_cell_pa_t_kernel(
         nc.gpsimd.tensor_copy(out=m[:], in_=mask_bf16[:])
 
         for k in range(N_BLOCKS + 2):
-            load_x(k + 2, 0, TILES)
-            load_small(k + 2)
-
             turn_x(k + 1, 0)
-            turn_x(k + 1, 1)
-            turn_back_cell(k - 1)
+            tb(k - 1, "f_rows")
             gate_step(k, 0)
+            turn_x(k + 1, 1)
             copy_x(k + 1, 0, nc.scalar.copy)
             cell_product(k - 1)
-            copy_x(k + 1, 1, nc.vector.tensor_copy)
-            gate_step(k, 1)
-            cell_state(k - 1)
-
             turn_x(k + 1, 2)
-            turn_x(k + 1, 3)
-            turn_back_last(k - 2)
-            gate_step(k, 2)
+            copy_x(k + 1, 1, nc.vector.tensor_copy)
+            tb(k - 1, "i_tanh_rows")
+            gate_step(k, 1)
+            load_x(k + 2, 0, TILES); load_small(k + 2)
             copy_x(k + 1, 2, nc.scalar.copy)
-            sums_s1_s2(k - 2)
+            cell_state(k - 1)
+            gate_step(k, 2)
+            tb(k - 2, "g1_rows")
+            turn_x(k + 1, 3)
+            tb(k - 2, "g2_rows")
+            sums1(k - 2)
             copy_x(k + 1, 3, nc.vector.tensor_copy)
+            sums2(k - 2)
             gate_step(k, 3)
+            cell_tanh(k - 1)
             output_s1(k - 2)
             gate_step(k, 4)
-            cell_tanh(k - 1)
-            output_s2(k - 2)
-            quantise_x(k + 1)
-
             turn_pair(k + 1, 0)
             turn_pair(k + 1, 1)
-            turn_back_first(k - 1)
-            gate_step(k, 5)
+            tb(k - 1, "o_rows")
             copy_pair(k + 1, 0)
+            quantise_x(k + 1)
+            gate_step(k, 5)
+            copy_pair(k + 1, 1)
+            tb(k - 1, "g0_rows")
             output_h(k - 1)
             gate_step(k, 6)
-            copy_pair(k + 1, 1)
+            output_s2(k - 2)
             output_s0(k - 1)

@@ -16,23 +16,21 @@ B = 4096
 DI = 1024
 DH = 128
 N_GATES = 7
-I_G = 0
-F_G = 1
-O_G = 2
-C_HAT = 3
-B0_G = 4
+COLS = N_GATES * DH
+I_G, F_G, O_G, C_HAT, B0_G = 0, 1, 2, 3, 4
 ROWS_PER_PARTITION = B // P
-TILES = 4
-BLOCK = TILES * P
-N_BLOCKS = B // BLOCK
-N_STEPS = N_BLOCKS * N_GATES
+PAIR = 2
+N_PAIRS = ROWS_PER_PARTITION // PAIR
+X_TILES = 4
 PACK = 4
 PASSES = DI // (P * PACK)
 HALVES = 2
-CHUNK = PASSES * P
 N_SMALL = 5
 C_SLOT = 4
-W_AHEAD = 2
+LEFT = slice(0, 3 * DH)
+RIGHT = slice(3 * DH, COLS)
+BANK = 512
+RUNS = ((0, 2), (2, 1), (3, 4))
 
 FLOPS = 2 * B * N_GATES * DH * (DI + DH)
 
@@ -44,66 +42,74 @@ def tile_share_lstm_cell_pa_t_kernel(
     out_0, out_1, out_2, out_3, out_4,
 ):
     nc = tc.nc
+    s_copy = nc.scalar.copy
+    v_copy = nc.vector.tensor_copy
 
     x_rows = x.rearrange("(p j) k -> p j k", j=ROWS_PER_PARTITION)
     small_rows = [
         a.rearrange("(p j) d -> p j d", j=ROWS_PER_PARTITION)
         for a in (h_minors, s0, s1, s2, c_minors)
     ]
-    h_dram, c_dram, s0_dram, s1_dram, s2_dram = [
-        a.rearrange("(p j) d -> p j d", j=ROWS_PER_PARTITION)
-        for a in (out_0, out_1, out_2, out_3, out_4)
-    ]
+    out_rows = {
+        name: a.rearrange("(p j) d -> p j d", j=ROWS_PER_PARTITION)
+        for name, a in (("h", out_0), ("c", out_1), ("s0", out_2), ("s1", out_3), ("s2", out_4))
+    }
 
     with ExitStack() as stack:
         stack.enter_context(tc.manual_schedule())
         const = stack.enter_context(tc.tile_pool(name="const", bufs=1))
         x_pool = stack.enter_context(tc.tile_pool(name="x_pool", bufs=3))
-        small_pool = stack.enter_context(tc.tile_pool(name="small_pool", bufs=4))
-        operand_pool = stack.enter_context(tc.tile_pool(name="operand_pool", bufs=2))
-        pre_pool = stack.enter_context(tc.tile_pool(name="pre_pool", bufs=4))
-        gate_pool = stack.enter_context(tc.tile_pool(name="gate_pool", bufs=2))
-        finish_pool = stack.enter_context(tc.tile_pool(name="finish_pool", bufs=2))
-        out_pool = stack.enter_context(tc.tile_pool(name="out_pool", bufs=2))
-        psum_in = stack.enter_context(tc.psum_pool(name="psum_in", bufs=3))
+        operand_pool = stack.enter_context(tc.tile_pool(name="operand_pool", bufs=3))
+        gate_pool = stack.enter_context(tc.tile_pool(name="gate_pool", bufs=4))
+        finish_pool = stack.enter_context(tc.tile_pool(name="finish_pool", bufs=3))
+        gated_pool = stack.enter_context(tc.tile_pool(name="gated_pool", bufs=1))
+        out_pool = stack.enter_context(tc.tile_pool(name="out_pool", bufs=3))
+        psum_turn = stack.enter_context(tc.psum_pool(name="psum_turn", bufs=3))
         psum_plain = stack.enter_context(tc.psum_pool(name="psum_plain", bufs=2))
         psum_mx = stack.enter_context(tc.psum_pool(name="psum_mx", bufs=3))
-        psum_back = psum_in
 
         held = {}
 
-        def live(k):
-            return 0 <= k < N_BLOCKS
+        def live(p):
+            return 0 <= p < N_PAIRS
 
-        def block_rows(k):
-            return slice(k * TILES, (k + 1) * TILES)
-
-        def load_x(k, first, count):
-            if not live(k):
-                return
-            if first == 0:
-                x_sb = x_pool.tile([P, TILES * DI], BF16, name="x_sb")
-                held["x_tiles", k] = x_sb[:].rearrange("p (t k) -> p t k", t=TILES)
-                held["x_words", k] = x_sb[:].bitcast(F32).rearrange("p (t w) -> p t w", t=TILES)
-            nc.sync.dma_start(
-                out=held["x_tiles", k][:, first:first + count, :],
-                in_=x_rows[:, k * TILES + first:k * TILES + first + count, :],
-            )
-
-        def load_small(k):
-            if not live(k):
-                return
-            small_sb = small_pool.tile([P, N_SMALL * TILES * DH], BF16, name="small_sb")
-            small = small_sb[:].rearrange("p (a t d) -> p a t d", a=N_SMALL, t=TILES)
-            for a in range(N_SMALL):
-                nc.sync.dma_start(out=small[:, a], in_=small_rows[a][:, block_rows(k), :])
-            held["small", k] = small
+        ident_f32 = const.tile([P, P], F32, name="ident_f32")
+        make_identity(nc, ident_f32[:])
+        ident_bf16 = const.tile([P, P], BF16, name="ident_bf16")
+        make_identity(nc, ident_bf16[:])
+        warm = const.tile([P, 1], F32, name="warm")
+        nc.vector.memset(warm[:], 0.0)
+        bias_rows = const.tile([P, COLS], BF16, name="bias_rows")
+        nc.vector.memset(bias_rows[:], 0.0)
+        ones = const.tile([P, P], BF16, name="ones")
+        nc.vector.memset(ones[:], 1.0)
 
         w_sb = const.tile([P, N_GATES * DI], BF16, name="w_sb")
+        w_tiles = w_sb[:].rearrange("p (c k) -> p c k", c=N_GATES)
         w_words = w_sb[:].bitcast(F32).rearrange("p (c w) -> p c w", c=N_GATES)
+        w_dram = weight_ih.rearrange("(c p) k -> p c k", p=P)
+        small_w = const.tile([P, N_GATES, DH], BF16, name="small_w")
+        small_all = const.tile([P, N_SMALL, ROWS_PER_PARTITION, DH], BF16, name="small_all")
+        mask_bf16 = const.tile([P, ROWS_PER_PARTITION], BF16, name="mask_bf16")
+
+        def load_x(block, first=0, count=X_TILES):
+            if not 0 <= block * X_TILES < ROWS_PER_PARTITION:
+                return
+            if first == 0:
+                x_sb = x_pool.tile([P, X_TILES * DI], BF16, name="x_sb")
+                held["x_tiles", block] = x_sb[:].rearrange("p (t k) -> p t k", t=X_TILES)
+                held["x_words", block] = x_sb[:].bitcast(F32).rearrange("p (t w) -> p t w", t=X_TILES)
+            row = block * X_TILES + first
+            nc.sync.dma_start(
+                out=held["x_tiles", block][:, first:first + count, :], in_=x_rows[:, row:row + count, :]
+            )
 
         def load_weights(c):
-            nc.sync.dma_start(out=w_sb[:, c * DI:(c + 1) * DI], in_=weight_ih[c * P:(c + 1) * P, :])
+            nc.sync.dma_start(out=w_tiles[:, c:c + 1, :], in_=w_dram[:, c:c + 1, :])
+
+        def load_small(first, end, tensors=range(N_SMALL)):
+            for a in tensors:
+                nc.sync.dma_start(out=small_all[:, a, first:end, :], in_=small_rows[a][:, first:end, :])
 
         def turn_words(words, pool, tag):
             turned = pool.tile([P, PASSES, HALVES, P], F32, name="turned", tag=tag)
@@ -113,339 +119,359 @@ def tile_share_lstm_cell_pa_t_kernel(
                     nc.tensor.transpose(turned[:, g, u, :], pass_words, ident_f32[:])
             return turned[:].rearrange("q g u r -> q g r u")
 
-        def turn_x(k, t):
-            if live(k):
-                held["x_ps", k, t] = turn_words(held["x_words", k][:, t, :], psum_in, "in")
+        def turn_x(p, t):
+            if live(p):
+                block, tile = divmod(p * PAIR + t, X_TILES)
+                held["x_ps", p, t] = turn_words(held["x_words", block][:, tile, :], psum_turn, "turn")
 
-        def copy_x(k, t, copy_out):
-            if not live(k):
+        def copy_x(p, t, copy_out):
+            if not live(p):
                 return
             if t == 0:
-                grouped = operand_pool.tile([P, PASSES * BLOCK * PACK], BF16, name="grouped", align_bytes=64)
-                held["grouped", k] = grouped
-            grouped_words = held["grouped", k][:].bitcast(F32).rearrange(
+                held["grouped", p] = operand_pool.tile(
+                    [P, PAIR * PASSES * P * PACK], BF16, name="grouped", align_bytes=64
+                )
+            words = held["grouped", p][:].bitcast(F32).rearrange(
+                "q (t g r u) -> q t g r u", t=PAIR, g=PASSES, u=HALVES
+            )
+            copy_out(out=words[:, t], in_=held["x_ps", p, t])
+
+        def quantise_x(p):
+            if not live(p):
+                return
+            held["x_codes", p] = operand_pool.tile([P, PAIR * PASSES * P], U32, name="x_codes", align_bytes=64)
+            held["x_scales", p] = operand_pool.tile([P, PAIR * PASSES * P], U8, name="x_scales", align_bytes=64)
+            nc.vector.quantize_mx(
+                out=held["x_codes", p][:].bitcast(FP8X4), scales=held["x_scales", p][:], in_=held["grouped", p][:]
+            )
+
+        def turn_small(p):
+            if not live(p):
+                return
+            small_ps = psum_turn.tile([P, PAIR, N_SMALL - 1, P], BF16, name="small_ps", tag="turn")
+            for t in range(PAIR):
+                for a in range(N_SMALL - 1):
+                    nc.tensor.transpose(small_ps[:, t, a, :], small_all[:, a, p * PAIR + t, :], ident_bf16[:])
+            held["small_ps", p] = small_ps
+
+        def copy_small(p):
+            if live(p):
+                turned = operand_pool.tile([P, PAIR, N_SMALL - 1, P], BF16, name="turned_small")
+                s_copy(out=turned[:], in_=held["small_ps", p][:])
+                held["turned_small", p] = turned
+
+        w_grouped = const.tile([P, PASSES * COLS * PACK], BF16, name="w_grouped", align_bytes=64)
+        w_codes = const.tile([P, PASSES * COLS], U32, name="w_codes", align_bytes=64)
+        w_scales = const.tile([P, PASSES * COLS], U8, name="w_scales", align_bytes=64)
+
+        def run_of(c):
+            for first, count in RUNS:
+                if first <= c < first + count:
+                    return PASSES * first * DH, count * DH, (c - first) * DH
+
+        def copy_weights(c, copy_out):
+            start, width, place = run_of(c)
+            words = w_grouped[:, start * PACK:(start + PASSES * width) * PACK].bitcast(F32).rearrange(
                 "q (g r u) -> q g r u", g=PASSES, u=HALVES
             )
-            copy_out(out=grouped_words[:, :, t * P:(t + 1) * P, :], in_=held["x_ps", k, t])
+            pool, tag = ((psum_mx, "mx"), (psum_plain, "plain"))[c % 2]
+            copy_out(out=words[:, :, place:place + DH, :], in_=turn_words(w_words[:, c, :], pool, tag))
 
-        def quantise_x(k):
-            if not live(k):
-                return
-            x_codes = operand_pool.tile([P, PASSES * BLOCK], U32, name="x_codes", align_bytes=64)
-            x_scales = operand_pool.tile([P, PASSES * BLOCK], U8, name="x_scales", align_bytes=64)
-            nc.vector.quantize_mx(
-                out=x_codes[:].bitcast(FP8X4), scales=x_scales[:], in_=held["grouped", k][:]
-            )
-            held["x_codes", k] = x_codes
-            held["x_scales", k] = x_scales
-
-        def turn_pair(k, pair):
-            if not live(k):
-                return
-            pair_ps = psum_in.tile([P, 2, TILES, P], BF16, name="pair_ps", tag="in")
-            for i in range(2):
-                for t in range(TILES):
-                    nc.tensor.transpose(
-                        pair_ps[:, i, t, :], held["small", k][:, 2 * pair + i, t, :], ident_bf16[:]
-                    )
-            held["pair_ps", k, pair] = pair_ps
-
-        def copy_pair(k, pair):
-            if not live(k):
-                return
-            if pair == 0:
-                turned_small = operand_pool.tile([P, (N_SMALL - 1) * BLOCK], BF16, name="turned_small")
-                held["turned_small", k] = turned_small[:].rearrange(
-                    "d (a r) -> d a r", a=N_SMALL - 1
-                )
-            nc.scalar.copy(
-                out=held["turned_small", k][:, 2 * pair:2 * pair + 2, :],
-                in_=held["pair_ps", k, pair][:].rearrange("d a t r -> d a (t r)"),
-            )
-
-        w_grouped = const.tile([P, N_GATES * CHUNK * PACK], BF16, name="w_grouped", align_bytes=64)
-        w_grouped_words = w_grouped[:].bitcast(F32).rearrange(
-            "q (c g r u) -> q c g r u", c=N_GATES, g=PASSES, u=HALVES
-        )
-        w_codes = const.tile([P, N_GATES * CHUNK], U32, name="w_codes", align_bytes=64)
-        w_scales = const.tile([P, N_GATES * CHUNK], U8, name="w_scales", align_bytes=64)
-
-        def prepare_weights(c):
-            copy_out = nc.scalar.copy if c % 2 == 0 else nc.vector.tensor_copy
-            copy_out(out=w_grouped_words[:, c], in_=turn_words(w_words[:, c, :], psum_back, "in"))
-            nc.vector.quantize_mx(
-                out=w_codes[:, c * CHUNK:(c + 1) * CHUNK].bitcast(FP8X4),
-                scales=w_scales[:, c * CHUNK:(c + 1) * CHUNK],
-                in_=w_grouped[:, c * CHUNK * PACK:(c + 1) * CHUNK * PACK],
-            )
-
-        def gate_matmuls(n):
-            if not 0 <= n < N_STEPS:
-                return
-            k, j = divmod(n, N_GATES)
-            plain = psum_plain.tile([P, BLOCK], F32, name="plain")
-            nc.tensor.matmul(
-                plain[:], lhsT=small_wT[:, j, :], rhs=held["turned_small", k][:, max(0, j - C_HAT), :],
-                start=True, stop=True,
-            )
-            acc = psum_mx.tile([P, BLOCK], F32, name="acc")
+        def quantise_weights(c):
+            start, width, place = run_of(c)
             for g in range(PASSES):
-                w_cols = slice(j * CHUNK + g * P, j * CHUNK + (g + 1) * P)
-                x_cols = slice(g * BLOCK, (g + 1) * BLOCK)
-                nc.tensor.matmul_mx(
-                    out=acc[:],
-                    lhsT=w_codes[:, w_cols].bitcast(FP8X4),
-                    lhsT_scale=w_scales[:, w_cols],
-                    rhs=held["x_codes", k][:, x_cols].bitcast(FP8X4),
-                    rhs_scale=held["x_scales", k][:, x_cols],
-                    start=(g == 0),
-                    stop=(g == PASSES - 1),
-                )
-            held["plain", n] = plain
-            held["acc", n] = acc
-
-        def gate_sum(n):
-            if not 0 <= n < N_STEPS:
-                return
-            pre = pre_pool.tile([P, BLOCK], F32, name="pre")
-            nc.scalar.copy(out=pre[:], in_=held["plain", n][:])
-            nc.vector.tensor_tensor(out=pre[:], in0=held["acc", n][:], in1=pre[:], op=ALU.add)
-            held["pre", n] = pre
-
-        def gate_function(n):
-            if not 0 <= n < N_STEPS:
-                return
-            k, j = divmod(n, N_GATES)
-            if j == 0:
-                held["gate", k] = gate_pool.tile([P, N_GATES, BLOCK], F32, name="gate")
-            if j == B0_G:
-                held["b_less_o", k] = gate_pool.tile([P, 3, BLOCK], F32, name="b_less_o")
-            gate = held["gate", k]
-            nc.scalar.activation(
-                out=gate[:, j, :], in_=held["pre", n][:], func=ACT.Tanh if j == C_HAT else ACT.Sigmoid,
-                bias=bias[:, j:j + 1],
-            )
-            if j == C_HAT:
-                i_tanh = gate_pool.tile([P, BLOCK], F32, name="i_tanh")
-                nc.gpsimd.tensor_tensor(out=i_tanh[:], in0=gate[:, I_G, :], in1=gate[:, C_HAT, :], op=ALU.mult)
-                held["i_tanh", k] = i_tanh
-            if j >= B0_G:
-                nc.gpsimd.tensor_tensor(
-                    out=held["b_less_o", k][:, j - B0_G, :], in0=gate[:, j, :], in1=gate[:, O_G, :],
-                    op=ALU.subtract,
+                cols = slice(start + g * width + place, start + g * width + place + DH)
+                nc.vector.quantize_mx(
+                    out=w_codes[:, cols].bitcast(FP8X4), scales=w_scales[:, cols],
+                    in_=w_grouped[:, cols.start * PACK:cols.stop * PACK],
                 )
 
-        def gate_step(k, j):
-            n = k * N_GATES + j
-            if n + W_AHEAD < N_GATES:
-                prepare_weights(n + W_AHEAD)
-            gate_matmuls(n)
-            gate_sum(n - 1)
-            gate_function(n - 2)
+        def bias_on_pe(cols, p, t):
+            return (p, t) != (0, 0) and (cols == RIGHT) == (t == 0)
 
-        def turn_back(k, name, features):
-            rows_ps = psum_back.tile([P, TILES, DH], F32, name="rows_ps", tag="in")
-            for t in range(TILES):
-                nc.tensor.transpose(rows_ps[:, t, :], features[:, t * P:(t + 1) * P], ident_f32[:])
-            held[name, k] = rows_ps
+        def plain(cols, p, t):
+            if not live(p):
+                return
+            bank = psum_plain.tile([P, BANK], F32, name="plain_ps", tag="plain")
+            turned = held["turned_small", p]
+            with_bias = bias_on_pe(cols, p, t)
+            width = cols.stop - cols.start
+            if with_bias:
+                nc.tensor.matmul(bank[:, 0:width], lhsT=ones[:], rhs=bias_rows[:, cols], start=True, stop=False)
+            if cols == LEFT:
+                products = [(0, 0, C_HAT)]
+            else:
+                products = [(a, C_HAT + a, C_HAT + a + 1) for a in range(N_SMALL - 1)]
+            for a, first, end in products:
+                place = first * DH - cols.start
+                nc.tensor.matmul(
+                    bank[:, place:place + (end - first) * DH], lhsT=turned[:, t, a, :],
+                    rhs=small_wT[:, first * DH:end * DH],
+                    start=not with_bias, stop=not with_bias or end * DH == cols.stop,
+                )
+            held["plain", cols.start, p, t] = bank
 
-        def tb(k, name):
-            if live(k):
-                if name == "f_rows": turn_back(k, name, held["gate", k][:, F_G, :])
-                elif name == "o_rows": turn_back(k, name, held["gate", k][:, O_G, :])
-                elif name == "i_tanh_rows": turn_back(k, name, held["i_tanh", k][:])
-                else: turn_back(k, name, held["b_less_o", k][:, int(name[1]), :])
-
-        def new_rows(pool, name, k):
-            held[name, k] = pool.tile([P, TILES, DH], F32, name=name)
-            return held[name, k]
-
-        def mask_of(k, t):
-            return m[:, k * TILES + t:k * TILES + t + 1]
-
-        def store(dram, k, name):
-            nc.sync.dma_start(out=dram[:, block_rows(k), :], in_=held[name, k][:])
-
-        def cell_product(k):
-            if live(k):
-                f_c = new_rows(finish_pool, "f_c", k)
-                for t in range(TILES):
-                    nc.vector.scalar_tensor_tensor(
-                        out=f_c[:, t, :], in0=held["f_rows", k][:, t, :], scalar=mask_of(k, t),
-                        in1=held["small", k][:, C_SLOT, t, :], op0=ALU.mult, op1=ALU.mult,
+        def mx(cols, p, t):
+            if not live(p):
+                return
+            bank = psum_mx.tile([P, BANK], F32, name="mx_ps", tag="mx")
+            for first, count in RUNS:
+                if not cols.start <= first * DH < cols.stop:
+                    continue
+                start, width, place = run_of(first)
+                for g in range(PASSES):
+                    x_cols = slice((t * PASSES + g) * P, (t * PASSES + g + 1) * P)
+                    w_cols = slice(start + g * width, start + (g + 1) * width)
+                    nc.tensor.matmul_mx(
+                        out=bank[:, first * DH - cols.start:(first + count) * DH - cols.start],
+                        lhsT=held["x_codes", p][:, x_cols].bitcast(FP8X4),
+                        lhsT_scale=held["x_scales", p][:, x_cols],
+                        rhs=w_codes[:, w_cols].bitcast(FP8X4),
+                        rhs_scale=w_scales[:, w_cols],
+                        start=(g == 0),
+                        stop=(g == PASSES - 1),
                     )
+            held["mx", cols.start, p, t] = bank
 
-        def cell_state(k):
-            if live(k):
-                c_out = new_rows(out_pool, "c_out", k)
-                for t in range(TILES):
-                    nc.vector.scalar_tensor_tensor(
-                        out=c_out[:, t, :], in0=held["i_tanh_rows", k][:, t, :], scalar=mask_of(k, t),
-                        in1=held["f_c", k][:, t, :], op0=ALU.mult, op1=ALU.add,
-                    )
+        def gate_tile(p):
+            if ("gates", p) not in held:
+                held["gates", p] = gate_pool.tile([P, PAIR, COLS], F32, name="gates")
+            return held["gates", p]
 
-        def cell_tanh(k):
-            if live(k):
-                tanh_c = new_rows(finish_pool, "tanh_c", k)
-                nc.scalar.activation(out=tanh_c[:], in_=held["c_out", k][:], func=ACT.Tanh)
-                tc_rows = new_rows(finish_pool, "tc_rows", k)
-                for t in range(TILES):
-                    nc.scalar.activation(
-                        out=tc_rows[:, t, :], in_=tanh_c[:, t, :], func=ACT.Copy, scale=mask_of(k, t)
-                    )
+        def fetch(cols, p, t):
+            if not live(p):
+                return
+            bank = held["plain", cols.start, p, t][:, 0:cols.stop - cols.start]
+            if bias_on_pe(cols, p, t):
+                s_copy(out=gate_tile(p)[:, t, cols], in_=bank)
+            else:
+                nc.vector.tensor_tensor(out=gate_tile(p)[:, t, cols], in0=bank, in1=bias_all[:, cols], op=ALU.add)
 
-        def output_h(k):
-            if live(k):
+        def add_mx(cols, p, t):
+            if live(p):
+                gates = gate_tile(p)[:, t, cols]
                 nc.vector.tensor_tensor(
-                    out=new_rows(out_pool, "h_out", k)[:], in0=held["o_rows", k][:], in1=held["tc_rows", k][:],
-                    op=ALU.mult,
+                    out=gates, in0=held["mx", cols.start, p, t][:, 0:cols.stop - cols.start], in1=gates, op=ALU.add
                 )
 
-        def output_s0(k):
-            if live(k):
+        def gate_function(func, first, end, p, t):
+            if live(p):
+                gates = gate_tile(p)[:, t, first * DH:end * DH]
+                nc.scalar.activation(out=gates, in_=gates, func=func)
+
+        def functions_left(p, t):
+            gate_function(ACT.Sigmoid, I_G, C_HAT, p, t)
+
+        def functions_right(p, t):
+            gate_function(ACT.Tanh, C_HAT, B0_G, p, t)
+            gate_function(ACT.Sigmoid, B0_G, N_GATES, p, t)
+
+        def gate(p, j):
+            return held["gates", p][:, :, j * DH:(j + 1) * DH]
+
+        def new_rows(pool, name, p):
+            held[name, p] = pool.tile([P, PAIR, DH], F32, name=name)
+            return held[name, p][:]
+
+        def mask_of(p, t):
+            return m[:, p * PAIR + t:p * PAIR + t + 1]
+
+        def cell_products(p, engine):
+            if live(p):
+                c_rows = small_all[:, C_SLOT, p * PAIR:(p + 1) * PAIR, :]
+                engine.tensor_tensor(out=new_rows(gated_pool, "i_tanh", p), in0=gate(p, I_G), in1=gate(p, C_HAT), op=ALU.mult)
+                engine.tensor_tensor(out=new_rows(finish_pool, "f_c", p), in0=gate(p, F_G), in1=c_rows, op=ALU.mult)
+
+        def gate_less_o(p, j, engine):
+            if live(p):
+                engine.tensor_tensor(
+                    out=new_rows(finish_pool, "g%d" % j, p), in0=gate(p, B0_G + j), in1=gate(p, O_G), op=ALU.subtract
+                )
+
+        def cell_sum(p):
+            if live(p):
+                nc.vector.tensor_tensor(
+                    out=new_rows(finish_pool, "cell", p), in0=held["f_c", p][:], in1=held["i_tanh", p][:], op=ALU.add
+                )
+
+        def masked(p, out, name, func):
+            for t in range(PAIR):
+                nc.scalar.activation(out=out[:, t, :], in_=held[name, p][:, t, :], func=func, scale=mask_of(p, t))
+
+        def cell_tanh(p):
+            if live(p):
+                masked(p, new_rows(finish_pool, "tanh_c", p), "cell", ACT.Tanh)
+                masked(p, new_rows(finish_pool, "tc", p), "tanh_c", ACT.Copy)
+
+        def output_c(p):
+            if live(p):
+                masked(p, new_rows(out_pool, "c", p), "cell", ACT.Copy)
+
+        def output_h(p):
+            if live(p):
+                nc.vector.tensor_tensor(out=new_rows(out_pool, "h", p), in0=gate(p, O_G), in1=held["tc", p][:], op=ALU.mult)
+
+        def combine(p, pool, name, in0, scalar, in1, op0, op1):
+            if live(p):
                 nc.vector.scalar_tensor_tensor(
-                    out=new_rows(out_pool, "s0_out", k)[:], in0=held["g0_rows", k][:], scalar=1.0,
-                    in1=held["tc_rows", k][:], op0=ALU.add, op1=ALU.mult,
-                )
-                store(h_dram, k, "h_out")
-                store(c_dram, k, "c_out")
-                store(s0_dram, k, "s0_out")
-
-        def sums1(k):
-            if live(k):
-                nc.vector.scalar_tensor_tensor(
-                    out=new_rows(finish_pool, "s1_sum", k)[:], in0=held["g1_rows", k][:], scalar=2.0,
-                    in1=held["s0_out", k][:], op0=ALU.add, op1=ALU.subtract,
+                    out=new_rows(pool, name, p), in0=held[in0, p][:], scalar=scalar, in1=held[in1, p][:], op0=op0, op1=op1
                 )
 
-        def sums2(k):
-            if live(k):
-                nc.vector.scalar_tensor_tensor(
-                    out=new_rows(finish_pool, "s2_part", k)[:], in0=held["s0_out", k][:], scalar=-2.0,
-                    in1=held["g2_rows", k][:], op0=ALU.mult, op1=ALU.add,
-                )
+        def output_s0(p):
+            combine(p, out_pool, "s0", "g0", 1.0, "tc", ALU.add, ALU.mult)
 
-        def output_s1(k):
-            if live(k):
-                nc.vector.scalar_tensor_tensor(
-                    out=new_rows(out_pool, "s1_out", k)[:], in0=held["s1_sum", k][:], scalar=0.5,
-                    in1=held["tc_rows", k][:], op0=ALU.mult, op1=ALU.mult,
-                )
-                nc.vector.scalar_tensor_tensor(
-                    out=new_rows(finish_pool, "s2_sum", k)[:], in0=held["s2_part", k][:], scalar=3.0,
-                    in1=held["s1_out", k][:], op0=ALU.add, op1=ALU.subtract,
-                )
+        def sum_s1(p):
+            combine(p, finish_pool, "sum1", "g1", 2.0, "s0", ALU.add, ALU.subtract)
 
-        def output_s2(k):
-            if live(k):
-                nc.vector.scalar_tensor_tensor(
-                    out=new_rows(out_pool, "s2_out", k)[:], in0=held["s2_sum", k][:], scalar=1.0 / 3.0,
-                    in1=held["tc_rows", k][:], op0=ALU.mult, op1=ALU.mult,
-                )
-                store(s1_dram, k, "s1_out")
-                store(s2_dram, k, "s2_out")
+        def part_s2(p):
+            combine(p, finish_pool, "part2", "s0", -2.0, "g2", ALU.mult, ALU.add)
 
-        ident_f32 = const.tile([P, P], F32, name="ident_f32")
-        make_identity(nc, ident_f32[:])
-        ident_bf16 = const.tile([P, P], BF16, name="ident_bf16")
-        make_identity(nc, ident_bf16[:])
+        def output_s1(p):
+            combine(p, out_pool, "s1", "sum1", 0.5, "tc", ALU.mult, ALU.mult)
 
-        small_w = const.tile([P, N_GATES, DH], BF16, name="small_w")
-        nc.scalar.dma_start(
-            out=small_w[:, 0:B0_G, :], in_=weight_hh.rearrange("(c p) d -> p c d", p=P)
-        )
+        def sum_s2(p):
+            combine(p, finish_pool, "sum2", "part2", 3.0, "s1", ALU.add, ALU.subtract)
+
+        def output_s2(p):
+            combine(p, out_pool, "s2", "sum2", 1.0 / 3.0, "tc", ALU.mult, ALU.mult)
+
+        def store(p, *names):
+            if live(p):
+                for name in names:
+                    nc.sync.dma_start(out=out_rows[name][:, p * PAIR:(p + 1) * PAIR, :], in_=held[name, p][:])
+
+        nc.scalar.dma_start(out=small_w[:, 0:B0_G, :], in_=weight_hh.rearrange("(c p) d -> p c d", p=P))
         for i, w in enumerate((weight_sh0, weight_sh1, weight_sh2)):
             nc.scalar.dma_start(out=small_w[:, B0_G + i, :], in_=w)
-        warm = const.tile([P, 1], F32, name="warm")
-        nc.vector.memset(warm[:], 0.0)
+        load_x(0, 0, 1)
+        load_x(0, 1, 1)
         nc.scalar.activation(out=warm[:], in_=warm[:], func=ACT.Sigmoid)
-
-        for t in range(TILES):
-            load_x(0, t, 1)
-        load_weights(0)
-        load_weights(1)
-        load_small(0)
-        bias_rows = const.tile([P, P], BF16, name="bias_rows")
-        nc.vector.memset(bias_rows[:], 0.0)
-        nc.gpsimd.dma_start(out=bias_rows[0:N_GATES, :], in_=bias_ih.rearrange("(r d) -> r d", d=DH))
-        nc.gpsimd.dma_start(
-            out=bias_rows[N_GATES:N_GATES + B0_G, :], in_=bias_hh.rearrange("(r d) -> r d", d=DH)
-        )
-        for i, b in enumerate((bias_sh0, bias_sh1, bias_sh2)):
-            row = N_GATES + B0_G + i
-            nc.gpsimd.dma_start(out=bias_rows[row:row + 1, :], in_=b.rearrange("(r d) -> r d", d=DH))
-        load_x(1, 0, 2)
-        load_weights(2)
-        load_weights(3)
-        load_x(1, 2, 2)
-        load_weights(4)
-        load_weights(5)
-        load_weights(6)
-        load_small(1)
-        mask_bf16 = const.tile([P, ROWS_PER_PARTITION], BF16, name="mask_bf16")
-        nc.gpsimd.dma_start(out=mask_bf16[:], in_=mask.rearrange("(p j) -> p j", j=ROWS_PER_PARTITION))
-
-        small_ps = psum_in.tile([P, N_GATES, P], BF16, name="small_ps", tag="in")
+        nc.scalar.dma_start(out=bias_rows[0:1, :], in_=bias_ih.rearrange("(r d) -> r d", r=1))
+        nc.scalar.dma_start(out=bias_rows[1:2, 0:B0_G * DH], in_=bias_hh.rearrange("(r d) -> r d", r=1))
         for c in range(N_GATES):
-            nc.tensor.transpose(small_ps[:, c, :], small_w[:, c, :], ident_bf16[:])
-        small_wT = const.tile([P, N_GATES, DH], BF16, name="small_wT")
-        nc.vector.tensor_copy(out=small_wT[:], in_=small_ps[:])
-
-        for t in range(TILES):
-            turn_x(0, t)
-            copy_x(0, t, nc.scalar.copy if t % 2 == 0 else nc.vector.tensor_copy)
-        quantise_x(0)
-        for c in range(W_AHEAD):
-            prepare_weights(c)
-        for pair in range(2):
-            turn_pair(0, pair)
-            copy_pair(0, pair)
-
-        bias_ps = psum_in.tile([P, P], BF16, name="bias_ps", tag="in")
-        nc.tensor.transpose(bias_ps[:], bias_rows[:], ident_bf16[:])
-        bias_cols = const.tile([P, 2 * N_GATES], F32, name="bias_cols")
-        nc.vector.tensor_copy(out=bias_cols[:], in_=bias_ps[:, 0:2 * N_GATES])
-        bias = const.tile([P, N_GATES], F32, name="bias")
-        nc.vector.tensor_tensor(
-            out=bias[:], in0=bias_cols[:, 0:N_GATES], in1=bias_cols[:, N_GATES:2 * N_GATES], op=ALU.add
-        )
+            load_weights(c)
+        load_small(0, PAIR, range(N_SMALL - 1))
+        load_x(0, 2, 1)
+        load_x(0, 3, 1)
+        load_small(PAIR, 8, range(N_SMALL - 1))
+        load_x(1)
+        load_small(0, 8, range(N_SMALL - 1, N_SMALL))
+        load_small(8, 16)
+        load_x(2)
+        for i, b in enumerate((bias_sh0, bias_sh1, bias_sh2)):
+            cols = slice((B0_G + i) * DH, (B0_G + i + 1) * DH)
+            nc.gpsimd.dma_start(out=bias_rows[1:2, cols], in_=b.rearrange("(r d) -> r d", r=1))
+        nc.gpsimd.dma_start(out=mask_bf16[:], in_=mask.rearrange("(p j) -> p j", j=ROWS_PER_PARTITION))
         m = const.tile([P, ROWS_PER_PARTITION], F32, name="m")
         nc.gpsimd.tensor_copy(out=m[:], in_=mask_bf16[:])
 
-        for k in range(N_BLOCKS + 2):
-            turn_x(k + 1, 0)
-            tb(k - 1, "f_rows")
-            gate_step(k, 0)
-            turn_x(k + 1, 1)
-            copy_x(k + 1, 0, nc.scalar.copy)
-            cell_product(k - 1)
-            turn_x(k + 1, 2)
-            copy_x(k + 1, 1, nc.vector.tensor_copy)
-            tb(k - 1, "i_tanh_rows")
-            gate_step(k, 1)
-            load_x(k + 2, 0, TILES); load_small(k + 2)
-            copy_x(k + 1, 2, nc.scalar.copy)
-            cell_state(k - 1)
-            gate_step(k, 2)
-            tb(k - 2, "g1_rows")
-            turn_x(k + 1, 3)
-            tb(k - 2, "g2_rows")
-            sums1(k - 2)
-            copy_x(k + 1, 3, nc.vector.tensor_copy)
-            sums2(k - 2)
-            gate_step(k, 3)
-            cell_tanh(k - 1)
-            output_s1(k - 2)
-            gate_step(k, 4)
-            turn_pair(k + 1, 0)
-            turn_pair(k + 1, 1)
-            tb(k - 1, "o_rows")
-            copy_pair(k + 1, 0)
-            quantise_x(k + 1)
-            gate_step(k, 5)
-            copy_pair(k + 1, 1)
-            tb(k - 1, "g0_rows")
-            output_h(k - 1)
-            gate_step(k, 6)
-            output_s2(k - 2)
-            output_s0(k - 1)
+        small_w_ps = psum_turn.tile([P, N_GATES, P], BF16, name="small_w_ps", tag="turn")
+        for c in range(N_GATES):
+            nc.tensor.transpose(small_w_ps[:, c, :], small_w[:, c, :], ident_bf16[:])
+        small_wT = const.tile([P, COLS], BF16, name="small_wT")
+        v_copy(out=small_wT[:], in_=small_w_ps[:].rearrange("d c f -> d (c f)"))
+        for t in range(PAIR):
+            turn_x(0, t)
+            copy_x(0, t, s_copy if t == 0 else v_copy)
+        quantise_x(0)
+        for c in range(N_GATES):
+            copy_weights(c, s_copy if c % 2 == 0 else v_copy)
+            if c > 0:
+                quantise_weights(c - 1)
+        bias_all = const.tile([P, COLS], F32, name="bias_all")
+        for cols in (LEFT, RIGHT):
+            bias_ps = psum_plain.tile([P, BANK], F32, name="bias_ps", tag="plain")
+            width = cols.stop - cols.start
+            nc.tensor.matmul(bias_ps[:, 0:width], lhsT=ones[:], rhs=bias_rows[:, cols], start=True, stop=True)
+            v_copy(out=bias_all[:, cols], in_=bias_ps[:, 0:width])
+        quantise_weights(N_GATES - 1)
+        turn_small(0)
+        copy_small(0)
+        for t in range(PAIR):
+            turn_x(1, t)
+            copy_x(1, t, s_copy if t == 0 else v_copy)
+        plain(LEFT, 0, 0)
+        plain(RIGHT, 0, 0)
+        fetch(RIGHT, 0, 0)
+        mx(RIGHT, 0, 0)
+        mx(LEFT, 0, 0)
+        turn_small(1)
+        copy_small(1)
+
+        for p in range(N_PAIRS):
+            if p == 0:
+                load_small(16, 32)
+            if p % 2 == 0:
+                load_x(p // 2 + 3)
+            fetch(LEFT, p, 0)
+            cell_tanh(p - 2)
+            plain(LEFT, p, 1)
+            mx(LEFT, p, 1)
+            fetch(LEFT, p, 1)
+            cell_products(p - 1, nc.gpsimd)
+            gate_less_o(p - 1, 0, nc.gpsimd)
+            gate_less_o(p - 1, 1, nc.gpsimd)
+            gate_less_o(p - 1, 2, nc.gpsimd)
+            add_mx(RIGHT, p, 0)
+            functions_right(p, 0)
+            plain(RIGHT, p, 1)
+            add_mx(LEFT, p, 0)
+            functions_left(p, 0)
+            mx(RIGHT, p, 1)
+            fetch(RIGHT, p, 1)
+            add_mx(LEFT, p, 1)
+            functions_left(p, 1)
+            add_mx(RIGHT, p, 1)
+            plain(RIGHT, p + 1, 0)
+            fetch(RIGHT, p + 1, 0)
+            turn_x(p + 2, 0)
+            turn_x(p + 2, 1)
+            turn_small(p + 2)
+            copy_x(p + 2, 0, s_copy)
+            copy_x(p + 2, 1, s_copy)
+            output_c(p - 2)
+            copy_small(p + 2)
+            functions_right(p, 1)
+            output_s0(p - 2)
+            output_h(p - 2)
+            sum_s1(p - 2)
+            part_s2(p - 2)
+            output_s1(p - 2)
+            cell_sum(p - 1)
+            sum_s2(p - 2)
+            if p == 0:
+                quantise_x(1)
+            quantise_x(p + 2)
+            output_s2(p - 2)
+            plain(LEFT, p + 1, 0)
+            mx(RIGHT, p + 1, 0)
+            mx(LEFT, p + 1, 0)
+            store(p - 2, "c", "h", "s0", "s1", "s2")
+
+        last = N_PAIRS - 1
+        cell_tanh(last - 1)
+        cell_products(last, nc.vector)
+        gate_less_o(last, 0, nc.vector)
+        cell_sum(last)
+        output_s0(last - 1)
+        output_h(last - 1)
+        cell_tanh(last)
+        output_c(last - 1)
+        output_c(last)
+        sum_s1(last - 1)
+        part_s2(last - 1)
+        output_s1(last - 1)
+        gate_less_o(last, 1, nc.vector)
+        sum_s2(last - 1)
+        gate_less_o(last, 2, nc.vector)
+        output_s2(last - 1)
+        store(last - 1, "c", "h", "s0", "s1", "s2")
+        output_s0(last)
+        output_h(last)
+        sum_s1(last)
+        part_s2(last)
+        output_s1(last)
+        store(last, "c", "h", "s0", "s1")
+        sum_s2(last)
+        output_s2(last)
+        store(last, "s2")

@@ -170,20 +170,19 @@ def tile_share_lstm_cell_pa_t_kernel(
                     return PASSES * first * DH, count * DH, (c - first) * DH
 
         def copy_weights(c, copy_out):
-            start, width, place = run_of(c)
-            words = w_grouped[:, start * PACK:(start + PASSES * width) * PACK].bitcast(F32).rearrange(
+            words = w_grouped[:, c * DI:(c + 1) * DI].bitcast(F32).rearrange(
                 "q (g r u) -> q g r u", g=PASSES, u=HALVES
             )
             pool, tag = ((psum_mx, "mx"), (psum_plain, "plain"))[c % 2]
-            copy_out(out=words[:, :, place:place + DH, :], in_=turn_words(w_words[:, c, :], pool, tag))
+            copy_out(out=words, in_=turn_words(w_words[:, c, :], pool, tag))
 
         def quantise_weights(c):
             start, width, place = run_of(c)
             for g in range(PASSES):
+                grouped = slice(c * DI + g * P * PACK, c * DI + (g + 1) * P * PACK)
                 cols = slice(start + g * width + place, start + g * width + place + DH)
                 nc.vector.quantize_mx(
-                    out=w_codes[:, cols].bitcast(FP8X4), scales=w_scales[:, cols],
-                    in_=w_grouped[:, cols.start * PACK:cols.stop * PACK],
+                    out=w_codes[:, cols].bitcast(FP8X4), scales=w_scales[:, cols], in_=w_grouped[:, grouped]
                 )
 
         def bias_on_pe(cols, p, t):
@@ -269,6 +268,9 @@ def tile_share_lstm_cell_pa_t_kernel(
         def gate(p, j):
             return held["gates", p][:, :, j * DH:(j + 1) * DH]
 
+        def rows_of(name, p):
+            return held[name, p][:]
+
         def new_rows(pool, name, p):
             held[name, p] = pool.tile([P, PAIR, DH], F32, name=name)
             return held[name, p][:]
@@ -276,17 +278,27 @@ def tile_share_lstm_cell_pa_t_kernel(
         def mask_of(p, t):
             return m[:, p * PAIR + t:p * PAIR + t + 1]
 
-        def cell_products(p, engine):
-            if live(p):
-                c_rows = small_all[:, C_SLOT, p * PAIR:(p + 1) * PAIR, :]
-                engine.tensor_tensor(out=new_rows(gated_pool, "i_tanh", p), in0=gate(p, I_G), in1=gate(p, C_HAT), op=ALU.mult)
-                engine.tensor_tensor(out=new_rows(finish_pool, "f_c", p), in0=gate(p, F_G), in1=c_rows, op=ALU.mult)
-
-        def gate_less_o(p, j, engine):
+        def input_product(p, engine):
             if live(p):
                 engine.tensor_tensor(
-                    out=new_rows(finish_pool, "g%d" % j, p), in0=gate(p, B0_G + j), in1=gate(p, O_G), op=ALU.subtract
+                    out=new_rows(gated_pool, "i_tanh", p), in0=gate(p, I_G), in1=gate(p, C_HAT), op=ALU.mult
                 )
+
+        def cell_product(p, engine):
+            if live(p):
+                c_rows = small_all[:, C_SLOT, p * PAIR:(p + 1) * PAIR, :]
+                engine.tensor_tensor(out=new_rows(finish_pool, "f_c", p), in0=gate(p, F_G), in1=c_rows, op=ALU.mult)
+
+        def gates_less_o(p, engine):
+            if live(p):
+                less_o = finish_pool.tile([P, PAIR, 3, DH], F32, name="less_o")
+                gates = held["gates", p][:].rearrange("p t (c d) -> p t c d", c=N_GATES)
+                engine.tensor_tensor(
+                    out=less_o[:], in0=gates[:, :, B0_G:N_GATES, :],
+                    in1=gates[:, :, O_G:O_G + 1, :].to_broadcast([P, PAIR, 3, DH]), op=ALU.subtract,
+                )
+                for j in range(3):
+                    held["g%d" % j, p] = less_o[:, :, j, :]
 
         def cell_sum(p):
             if live(p):
@@ -314,7 +326,7 @@ def tile_share_lstm_cell_pa_t_kernel(
         def combine(p, pool, name, in0, scalar, in1, op0, op1):
             if live(p):
                 nc.vector.scalar_tensor_tensor(
-                    out=new_rows(pool, name, p), in0=held[in0, p][:], scalar=scalar, in1=held[in1, p][:], op0=op0, op1=op1
+                    out=new_rows(pool, name, p), in0=rows_of(in0, p), scalar=scalar, in1=rows_of(in1, p), op0=op0, op1=op1
                 )
 
         def output_s0(p):
@@ -408,10 +420,8 @@ def tile_share_lstm_cell_pa_t_kernel(
             plain(LEFT, p, 1)
             mx(LEFT, p, 1)
             fetch(LEFT, p, 1)
-            cell_products(p - 1, nc.gpsimd)
-            gate_less_o(p - 1, 0, nc.gpsimd)
-            gate_less_o(p - 1, 1, nc.gpsimd)
-            gate_less_o(p - 1, 2, nc.gpsimd)
+            input_product(p - 1, nc.gpsimd)
+            gates_less_o(p - 1, nc.gpsimd)
             add_mx(RIGHT, p, 0)
             functions_right(p, 0)
             plain(RIGHT, p, 1)
@@ -435,6 +445,7 @@ def tile_share_lstm_cell_pa_t_kernel(
             output_s0(p - 2)
             output_h(p - 2)
             sum_s1(p - 2)
+            cell_product(p - 1, nc.vector)
             part_s2(p - 2)
             output_s1(p - 2)
             cell_sum(p - 1)
@@ -450,8 +461,9 @@ def tile_share_lstm_cell_pa_t_kernel(
 
         last = N_PAIRS - 1
         cell_tanh(last - 1)
-        cell_products(last, nc.vector)
-        gate_less_o(last, 0, nc.vector)
+        input_product(last, nc.vector)
+        cell_product(last, nc.vector)
+        gates_less_o(last, nc.vector)
         cell_sum(last)
         output_s0(last - 1)
         output_h(last - 1)
@@ -461,9 +473,7 @@ def tile_share_lstm_cell_pa_t_kernel(
         sum_s1(last - 1)
         part_s2(last - 1)
         output_s1(last - 1)
-        gate_less_o(last, 1, nc.vector)
         sum_s2(last - 1)
-        gate_less_o(last, 2, nc.vector)
         output_s2(last - 1)
         store(last - 1, "c", "h", "s0", "s1", "s2")
         output_s0(last)

@@ -108,6 +108,8 @@ def tile_share_lstm_cell_pa_t_kernel(
             nc.sync.dma_start(out=w_tiles[:, c:c + 1, :], in_=w_dram[:, c:c + 1, :])
 
         def load_small(first, end, tensors=range(N_SMALL)):
+            if end > ROWS_PER_PARTITION:
+                return
             for a in tensors:
                 nc.sync.dma_start(out=small_all[:, a, first:end, :], in_=small_rows[a][:, first:end, :])
 
@@ -186,7 +188,7 @@ def tile_share_lstm_cell_pa_t_kernel(
                 )
 
         def bias_on_pe(cols, p, t):
-            return (p, t) != (0, 0) and (cols == RIGHT) == (t == 0)
+            return cols == RIGHT and (p > 2 or (p == 2 and t == 1))
 
         def plain(cols, p, t):
             if not live(p):
@@ -365,11 +367,10 @@ def tile_share_lstm_cell_pa_t_kernel(
         load_small(0, PAIR, range(N_SMALL - 1))
         load_x(0, 2, 1)
         load_x(0, 3, 1)
-        load_small(PAIR, 8, range(N_SMALL - 1))
+        load_small(PAIR, X_TILES, range(N_SMALL - 1))
         load_x(1)
-        load_small(0, 8, range(N_SMALL - 1, N_SMALL))
-        load_small(8, 16)
-        load_x(2)
+        load_small(X_TILES, 2 * X_TILES, range(N_SMALL - 1))
+        load_small(0, 2 * X_TILES, range(N_SMALL - 1, N_SMALL))
         for i, b in enumerate((bias_sh0, bias_sh1, bias_sh2)):
             cols = slice((B0_G + i) * DH, (B0_G + i + 1) * DH)
             nc.gpsimd.dma_start(out=bias_rows[1:2, cols], in_=b.rearrange("(r d) -> r d", r=1))
@@ -377,33 +378,35 @@ def tile_share_lstm_cell_pa_t_kernel(
         m = const.tile([P, ROWS_PER_PARTITION], F32, name="m")
         nc.gpsimd.tensor_copy(out=m[:], in_=mask_bf16[:])
 
-        small_w_ps = psum_turn.tile([P, N_GATES, P], BF16, name="small_w_ps", tag="turn")
-        for c in range(N_GATES):
-            nc.tensor.transpose(small_w_ps[:, c, :], small_w[:, c, :], ident_bf16[:])
-        small_wT = const.tile([P, COLS], BF16, name="small_wT")
-        v_copy(out=small_wT[:], in_=small_w_ps[:].rearrange("d c f -> d (c f)"))
         for t in range(PAIR):
             turn_x(0, t)
             copy_x(0, t, s_copy if t == 0 else v_copy)
         quantise_x(0)
+        small_wT = const.tile([P, COLS], BF16, name="small_wT")
         for c in range(N_GATES):
-            copy_weights(c, s_copy if c % 2 == 0 else v_copy)
+            copy_weights(c, v_copy if c in (1, 3) else s_copy)
             if c > 0:
                 quantise_weights(c - 1)
+            if c == 1:
+                small_w_ps = psum_turn.tile([P, N_GATES, P], BF16, name="small_w_ps", tag="turn")
+                for i in range(N_GATES):
+                    nc.tensor.transpose(small_w_ps[:, i, :], small_w[:, i, :], ident_bf16[:])
+                s_copy(out=small_wT[:], in_=small_w_ps[:].rearrange("d c f -> d (c f)"))
+        turn_small(0)
+        copy_small(0)
+        quantise_weights(N_GATES - 1)
         bias_all = const.tile([P, COLS], F32, name="bias_all")
         for cols in (LEFT, RIGHT):
             bias_ps = psum_plain.tile([P, BANK], F32, name="bias_ps", tag="plain")
             width = cols.stop - cols.start
             nc.tensor.matmul(bias_ps[:, 0:width], lhsT=ones[:], rhs=bias_rows[:, cols], start=True, stop=True)
             v_copy(out=bias_all[:, cols], in_=bias_ps[:, 0:width])
-        quantise_weights(N_GATES - 1)
-        turn_small(0)
-        copy_small(0)
         for t in range(PAIR):
             turn_x(1, t)
             copy_x(1, t, s_copy if t == 0 else v_copy)
         plain(LEFT, 0, 0)
         plain(RIGHT, 0, 0)
+        fetch(LEFT, 0, 0)
         fetch(RIGHT, 0, 0)
         mx(RIGHT, 0, 0)
         mx(LEFT, 0, 0)
@@ -411,48 +414,54 @@ def tile_share_lstm_cell_pa_t_kernel(
         copy_small(1)
 
         for p in range(N_PAIRS):
-            if p == 0:
-                load_small(16, 32)
             if p % 2 == 0:
-                load_x(p // 2 + 3)
-            fetch(LEFT, p, 0)
-            cell_tanh(p - 2)
+                load_x(p // 2 + 2)
+                load_small((p // 2 + 2) * X_TILES, (p // 2 + 3) * X_TILES)
+            if p > 0:
+                fetch(LEFT, p, 0)
+            plain(RIGHT, p, 1)
+            mx(RIGHT, p, 1)
             plain(LEFT, p, 1)
-            mx(LEFT, p, 1)
-            fetch(LEFT, p, 1)
+            cell_tanh(p - 2)
+            fetch(RIGHT, p, 1)
             input_product(p - 1, nc.gpsimd)
             gates_less_o(p - 1, nc.gpsimd)
             add_mx(RIGHT, p, 0)
             functions_right(p, 0)
-            plain(RIGHT, p, 1)
+            output_c(p - 2)
             add_mx(LEFT, p, 0)
             functions_left(p, 0)
-            mx(RIGHT, p, 1)
-            fetch(RIGHT, p, 1)
-            add_mx(LEFT, p, 1)
-            functions_left(p, 1)
+            mx(LEFT, p, 1)
+            fetch(LEFT, p, 1)
             add_mx(RIGHT, p, 1)
-            plain(RIGHT, p + 1, 0)
-            fetch(RIGHT, p + 1, 0)
+            if p == 0:
+                quantise_x(1)
+            add_mx(LEFT, p, 1)
+            if p < 2:
+                plain(RIGHT, p + 1, 0)
+            if p < 2:
+                fetch(RIGHT, p + 1, 0)
             turn_x(p + 2, 0)
             turn_x(p + 2, 1)
             turn_small(p + 2)
             copy_x(p + 2, 0, s_copy)
             copy_x(p + 2, 1, s_copy)
-            output_c(p - 2)
-            copy_small(p + 2)
+            if p >= 2:
+                plain(RIGHT, p + 1, 0)
+            functions_left(p, 1)
+            if p >= 2:
+                fetch(RIGHT, p + 1, 0)
             functions_right(p, 1)
+            copy_small(p + 2)
             output_s0(p - 2)
-            output_h(p - 2)
-            sum_s1(p - 2)
             cell_product(p - 1, nc.vector)
+            sum_s1(p - 2)
             part_s2(p - 2)
             output_s1(p - 2)
-            cell_sum(p - 1)
+            output_h(p - 2)
             sum_s2(p - 2)
-            if p == 0:
-                quantise_x(1)
             quantise_x(p + 2)
+            cell_sum(p - 1)
             output_s2(p - 2)
             plain(LEFT, p + 1, 0)
             mx(RIGHT, p + 1, 0)

@@ -423,10 +423,13 @@ def tile_share_lstm_cell_pa_t_kernel(
             mx(RIGHT, p, 1)
             plain(LEFT, p, 1)
             cell_tanh(p - 2)
-            fetch(RIGHT, p, 1)
+            if bias_on_pe(RIGHT, p, 1):
+                fetch(RIGHT, p, 1)
             input_product(p - 1, nc.gpsimd)
             gates_less_o(p - 1, nc.gpsimd)
             add_mx(RIGHT, p, 0)
+            if not bias_on_pe(RIGHT, p, 1):
+                fetch(RIGHT, p, 1)
             functions_right(p, 0)
             output_c(p - 2)
             add_mx(LEFT, p, 0)
@@ -474,23 +477,24 @@ def tile_share_lstm_cell_pa_t_kernel(
         cell_product(last, nc.vector)
         gates_less_o(last, nc.vector)
         cell_sum(last)
+        cell_tanh(last)
         output_s0(last - 1)
         output_h(last - 1)
-        cell_tanh(last)
         output_c(last - 1)
         output_c(last)
         sum_s1(last - 1)
         part_s2(last - 1)
         output_s1(last - 1)
+        output_s0(last)
         sum_s2(last - 1)
+        output_h(last)
         output_s2(last - 1)
         store(last - 1, "c", "h", "s0", "s1", "s2")
-        output_s0(last)
-        output_h(last)
+        store(last, "c", "h", "s0")
         sum_s1(last)
         part_s2(last)
         output_s1(last)
-        store(last, "c", "h", "s0", "s1")
+        store(last, "s1")
         sum_s2(last)
         output_s2(last)
         store(last, "s2")

@@ -349,6 +349,22 @@ def tile_share_lstm_cell_pa_t_kernel(
         def output_s2(p):
             combine(p, out_pool, "s2", "sum2", 1.0 / 3.0, "tc", ALU.mult, ALU.mult)
 
+        def finish_s2(p):
+            total = new_rows(finish_pool, "sum2", p)
+            s2_out = new_rows(out_pool, "s2", p)
+            for t in range(PAIR):
+                nc.vector.scalar_tensor_tensor(
+                    out=total[:, t, :], in0=rows_of("part2", p)[:, t, :], scalar=3.0, in1=rows_of("s1", p)[:, t, :],
+                    op0=ALU.add, op1=ALU.subtract,
+                )
+            for t in range(PAIR):
+                nc.vector.scalar_tensor_tensor(
+                    out=s2_out[:, t, :], in0=total[:, t, :], scalar=1.0 / 3.0, in1=rows_of("tc", p)[:, t, :],
+                    op0=ALU.mult, op1=ALU.mult,
+                )
+                row = p * PAIR + t
+                nc.sync.dma_start(out=out_rows["s2"][:, row:row + 1, :], in_=s2_out[:, t:t + 1, :])
+
         def store(p, *names):
             if live(p):
                 for name in names:
@@ -400,10 +416,10 @@ def tile_share_lstm_cell_pa_t_kernel(
             bias_ps = psum_plain.tile([P, BANK], F32, name="bias_ps", tag="plain")
             width = cols.stop - cols.start
             nc.tensor.matmul(bias_ps[:, 0:width], lhsT=ones[:], rhs=bias_rows[:, cols], start=True, stop=True)
-            v_copy(out=bias_all[:, cols], in_=bias_ps[:, 0:width])
+            s_copy(out=bias_all[:, cols], in_=bias_ps[:, 0:width])
         for t in range(PAIR):
             turn_x(1, t)
-            copy_x(1, t, s_copy if t == 0 else v_copy)
+            copy_x(1, t, s_copy)
         plain(LEFT, 0, 0)
         plain(RIGHT, 0, 0)
         fetch(LEFT, 0, 0)
@@ -477,24 +493,28 @@ def tile_share_lstm_cell_pa_t_kernel(
         cell_product(last, nc.vector)
         gates_less_o(last, nc.vector)
         cell_sum(last)
-        cell_tanh(last)
-        output_s0(last - 1)
-        output_h(last - 1)
         output_c(last - 1)
+        store(last - 1, "c")
+        cell_tanh(last)
         output_c(last)
+        output_s0(last - 1)
+        store(last - 1, "s0")
+        output_h(last - 1)
+        store(last - 1, "h")
         sum_s1(last - 1)
         part_s2(last - 1)
+        store(last, "c")
         output_s1(last - 1)
+        store(last - 1, "s1")
         output_s0(last)
+        store(last, "s0")
         sum_s2(last - 1)
         output_h(last)
+        store(last, "h")
         output_s2(last - 1)
-        store(last - 1, "c", "h", "s0", "s1", "s2")
-        store(last, "c", "h", "s0")
+        store(last - 1, "s2")
         sum_s1(last)
         part_s2(last)
         output_s1(last)
         store(last, "s1")
-        sum_s2(last)
-        output_s2(last)
-        store(last, "s2")
+        finish_s2(last)

@@ -462,11 +462,11 @@ def tile_share_lstm_cell_pa_t_kernel(
                 fetch(RIGHT, p + 1, 0)
             turn_x(p + 2, 0)
             turn_x(p + 2, 1)
-            turn_small(p + 2)
             copy_x(p + 2, 0, s_copy)
             copy_x(p + 2, 1, s_copy)
             if p >= 2:
                 plain(RIGHT, p + 1, 0)
+            turn_small(p + 2)
             functions_left(p, 1)
             if p >= 2:
                 fetch(RIGHT, p + 1, 0)

@@ -416,7 +416,7 @@ def tile_share_lstm_cell_pa_t_kernel(
             bias_ps = psum_plain.tile([P, BANK], F32, name="bias_ps", tag="plain")
             width = cols.stop - cols.start
             nc.tensor.matmul(bias_ps[:, 0:width], lhsT=ones[:], rhs=bias_rows[:, cols], start=True, stop=True)
-            s_copy(out=bias_all[:, cols], in_=bias_ps[:, 0:width])
+            v_copy(out=bias_all[:, cols], in_=bias_ps[:, 0:width])
         for t in range(PAIR):
             turn_x(1, t)
             copy_x(1, t, s_copy)

from contextlib import ExitStack

import concourse.mybir as mybir
from concourse.masks import make_identity

F32 = mybir.dt.float32
BF16 = mybir.dt.bfloat16
U32 = mybir.dt.uint32
U8 = mybir.dt.uint8
FP8X4 = mybir.dt.float8_e4m3fn_x4
ACT = mybir.ActivationFunctionType
ALU = mybir.AluOpType

P = 128
B = 4096
DI = 1024
DH = 128
N_GATES = 7
COLS = N_GATES * DH
I_G, F_G, O_G, C_HAT, B0_G = 0, 1, 2, 3, 4
ROWS_PER_PARTITION = B // P
PAIR = 2
N_PAIRS = ROWS_PER_PARTITION // PAIR
X_TILES = 4
PACK = 4
PASSES = DI // (P * PACK)
HALVES = 2
N_SMALL = 5
C_SLOT = 4
LEFT = slice(0, 3 * DH)
RIGHT = slice(3 * DH, COLS)
BANK = 512
RUNS = ((0, 2), (2, 1), (3, 4))

FLOPS = 2 * B * N_GATES * DH * (DI + DH)


def tile_share_lstm_cell_pa_t_kernel(
    tc, x, h_minors, c_minors, s0, s1, s2, mask,
    weight_ih, bias_ih, weight_hh, bias_hh,
    weight_sh0, bias_sh0, weight_sh1, bias_sh1, weight_sh2, bias_sh2,
    out_0, out_1, out_2, out_3, out_4,
):
    nc = tc.nc
    s_copy = nc.scalar.copy
    v_copy = nc.vector.tensor_copy

    x_rows = x.rearrange("(p j) k -> p j k", j=ROWS_PER_PARTITION)
    small_rows = [
        a.rearrange("(p j) d -> p j d", j=ROWS_PER_PARTITION)
        for a in (h_minors, s0, s1, s2, c_minors)
    ]
    out_rows = {
        name: a.rearrange("(p j) d -> p j d", j=ROWS_PER_PARTITION)
        for name, a in (("h", out_0), ("c", out_1), ("s0", out_2), ("s1", out_3), ("s2", out_4))
    }

    with ExitStack() as stack:
        stack.enter_context(tc.manual_schedule())
        const = stack.enter_context(tc.tile_pool(name="const", bufs=1))
        x_pool = stack.enter_context(tc.tile_pool(name="x_pool", bufs=3))
        operand_pool = stack.enter_context(tc.tile_pool(name="operand_pool", bufs=3))
        gate_pool = stack.enter_context(tc.tile_pool(name="gate_pool", bufs=4))
        finish_pool = stack.enter_context(tc.tile_pool(name="finish_pool", bufs=3))
        gated_pool = stack.enter_context(tc.tile_pool(name="gated_pool", bufs=1))
        out_pool = stack.enter_context(tc.tile_pool(name="out_pool", bufs=3))
        psum_turn = stack.enter_context(tc.psum_pool(name="psum_turn", bufs=3))
        psum_plain = stack.enter_context(tc.psum_pool(name="psum_plain", bufs=2))
        psum_mx = stack.enter_context(tc.psum_pool(name="psum_mx", bufs=3))

        held = {}

        def live(p):
            return 0 <= p < N_PAIRS

        ident_f32 = const.tile([P, P], F32, name="ident_f32")
        make_identity(nc, ident_f32[:])
        ident_bf16 = const.tile([P, P], BF16, name="ident_bf16")
        make_identity(nc, ident_bf16[:])
        warm = const.tile([P, 1], F32, name="warm")
        nc.vector.memset(warm[:], 0.0)
        bias_rows = const.tile([P, COLS], BF16, name="bias_rows")
        nc.vector.memset(bias_rows[:], 0.0)
        ones = const.tile([P, P], BF16, name="ones")
        nc.vector.memset(ones[:], 1.0)

        w_sb = const.tile([P, N_GATES * DI], BF16, name="w_sb")
        w_tiles = w_sb[:].rearrange("p (c k) -> p c k", c=N_GATES)
        w_words = w_sb[:].bitcast(F32).rearrange("p (c w) -> p c w", c=N_GATES)
        w_dram = weight_ih.rearrange("(c p) k -> p c k", p=P)
        small_w = const.tile([P, N_GATES, DH], BF16, name="small_w")
        small_all = const.tile([P, N_SMALL, ROWS_PER_PARTITION, DH], BF16, name="small_all")
        mask_bf16 = const.tile([P, ROWS_PER_PARTITION], BF16, name="mask_bf16")

        def load_x(block, first=0, count=X_TILES):
            if not 0 <= block * X_TILES < ROWS_PER_PARTITION:
                return
            if first == 0:
                x_sb = x_pool.tile([P, X_TILES * DI], BF16, name="x_sb")
                held["x_tiles", block] = x_sb[:].rearrange("p (t k) -> p t k", t=X_TILES)
                held["x_words", block] = x_sb[:].bitcast(F32).rearrange("p (t w) -> p t w", t=X_TILES)
            row = block * X_TILES + first
            nc.sync.dma_start(
                out=held["x_tiles", block][:, first:first + count, :], in_=x_rows[:, row:row + count, :]
            )

        def load_weights(c):
            nc.sync.dma_start(out=w_tiles[:, c:c + 1, :], in_=w_dram[:, c:c + 1, :])

        def load_small(first, end, tensors=range(N_SMALL)):
            if end > ROWS_PER_PARTITION:
                return
            for a in tensors:
                nc.sync.dma_start(out=small_all[:, a, first:end, :], in_=small_rows[a][:, first:end, :])

        def turn_words(words, pool, tag):
            turned = pool.tile([P, PASSES, HALVES, P], F32, name="turned", tag=tag)
            for g in range(PASSES):
                for u in range(HALVES):
                    pass_words = words[:, g * HALVES * P + u:(g + 1) * HALVES * P:HALVES]
                    nc.tensor.transpose(turned[:, g, u, :], pass_words, ident_f32[:])
            return turned[:].rearrange("q g u r -> q g r u")

        def turn_x(p, t):
            if live(p):
                block, tile = divmod(p * PAIR + t, X_TILES)
                held["x_ps", p, t] = turn_words(held["x_words", block][:, tile, :], psum_turn, "turn")

        def copy_x(p, t, copy_out):
            if not live(p):
                return
            if t == 0:
                held["grouped", p] = operand_pool.tile(
                    [P, PAIR * PASSES * P * PACK], BF16, name="grouped", align_bytes=64
                )
            words = held["grouped", p][:].bitcast(F32).rearrange(
                "q (t g r u) -> q t g r u", t=PAIR, g=PASSES, u=HALVES
            )
            copy_out(out=words[:, t], in_=held["x_ps", p, t])

        def quantise_x(p):
            if not live(p):
                return
            held["x_codes", p] = operand_pool.tile([P, PAIR * PASSES * P], U32, name="x_codes", align_bytes=64)
            held["x_scales", p] = operand_pool.tile([P, PAIR * PASSES * P], U8, name="x_scales", align_bytes=64)
            nc.vector.quantize_mx(
                out=held["x_codes", p][:].bitcast(FP8X4), scales=held["x_scales", p][:], in_=held["grouped", p][:]
            )

        def turn_small(p):
            if not live(p):
                return
            small_ps = psum_turn.tile([P, PAIR, N_SMALL - 1, P], BF16, name="small_ps", tag="turn")
            for t in range(PAIR):
                for a in range(N_SMALL - 1):
                    nc.tensor.transpose(small_ps[:, t, a, :], small_all[:, a, p * PAIR + t, :], ident_bf16[:])
            held["small_ps", p] = small_ps

        def copy_small(p):
            if live(p):
                turned = operand_pool.tile([P, PAIR, N_SMALL - 1, P], BF16, name="turned_small")
                s_copy(out=turned[:], in_=held["small_ps", p][:])
                held["turned_small", p] = turned

        w_grouped = const.tile([P, PASSES * COLS * PACK], BF16, name="w_grouped", align_bytes=64)
        w_codes = const.tile([P, PASSES * COLS], U32, name="w_codes", align_bytes=64)
        w_scales = const.tile([P, PASSES * COLS], U8, name="w_scales", align_bytes=64)

        def run_of(c):
            for first, count in RUNS:
                if first <= c < first + count:
                    return PASSES * first * DH, count * DH, (c - first) * DH

        def copy_weights(c, copy_out):
            words = w_grouped[:, c * DI:(c + 1) * DI].bitcast(F32).rearrange(
                "q (g r u) -> q g r u", g=PASSES, u=HALVES
            )
            pool, tag = ((psum_mx, "mx"), (psum_plain, "plain"))[c % 2]
            copy_out(out=words, in_=turn_words(w_words[:, c, :], pool, tag))

        def quantise_weights(c):
            start, width, place = run_of(c)
            for g in range(PASSES):
                grouped = slice(c * DI + g * P * PACK, c * DI + (g + 1) * P * PACK)
                cols = slice(start + g * width + place, start + g * width + place + DH)
                nc.vector.quantize_mx(
                    out=w_codes[:, cols].bitcast(FP8X4), scales=w_scales[:, cols], in_=w_grouped[:, grouped]
                )

        def bias_on_pe(cols, p, t):
            return cols == RIGHT and (p > 2 or (p == 2 and t == 1))

        def plain(cols, p, t):
            if not live(p):
                return
            bank = psum_plain.tile([P, BANK], F32, name="plain_ps", tag="plain")
            turned = held["turned_small", p]
            with_bias = bias_on_pe(cols, p, t)
            width = cols.stop - cols.start
            if with_bias:
                nc.tensor.matmul(bank[:, 0:width], lhsT=ones[:], rhs=bias_rows[:, cols], start=True, stop=False)
            if cols == LEFT:
                products = [(0, 0, C_HAT)]
            else:
                products = [(a, C_HAT + a, C_HAT + a + 1) for a in range(N_SMALL - 1)]
            for a, first, end in products:
                place = first * DH - cols.start
                nc.tensor.matmul(
                    bank[:, place:place + (end - first) * DH], lhsT=turned[:, t, a, :],
                    rhs=small_wT[:, first * DH:end * DH],
                    start=not with_bias, stop=not with_bias or end * DH == cols.stop,
                )
            held["plain", cols.start, p, t] = bank

        def mx(cols, p, t):
            if not live(p):
                return
            bank = psum_mx.tile([P, BANK], F32, name="mx_ps", tag="mx")
            for first, count in RUNS:
                if not cols.start <= first * DH < cols.stop:
                    continue
                start, width, place = run_of(first)
                for g in range(PASSES):
                    x_cols = slice((t * PASSES + g) * P, (t * PASSES + g + 1) * P)
                    w_cols = slice(start + g * width, start + (g + 1) * width)
                    nc.tensor.matmul_mx(
                        out=bank[:, first * DH - cols.start:(first + count) * DH - cols.start],
                        lhsT=held["x_codes", p][:, x_cols].bitcast(FP8X4),
                        lhsT_scale=held["x_scales", p][:, x_cols],
                        rhs=w_codes[:, w_cols].bitcast(FP8X4),
                        rhs_scale=w_scales[:, w_cols],
                        start=(g == 0),
                        stop=(g == PASSES - 1),
                    )
            held["mx", cols.start, p, t] = bank

        def gate_tile(p):
            if ("gates", p) not in held:
                held["gates", p] = gate_pool.tile([P, PAIR, COLS], F32, name="gates")
            return held["gates", p]

        def fetch(cols, p, t):
            if not live(p):
                return
            bank = held["plain", cols.start, p, t][:, 0:cols.stop - cols.start]
            if bias_on_pe(cols, p, t):
                s_copy(out=gate_tile(p)[:, t, cols], in_=bank)
            else:
                nc.vector.tensor_tensor(out=gate_tile(p)[:, t, cols], in0=bank, in1=bias_all[:, cols], op=ALU.add)

        def add_mx(cols, p, t):
            if live(p):
                gates = gate_tile(p)[:, t, cols]
                nc.vector.tensor_tensor(
                    out=gates, in0=held["mx", cols.start, p, t][:, 0:cols.stop - cols.start], in1=gates, op=ALU.add
                )

        def gate_function(func, first, end, p, t):
            if live(p):
                gates = gate_tile(p)[:, t, first * DH:end * DH]
                nc.scalar.activation(out=gates, in_=gates, func=func)

        def functions_left(p, t):
            gate_function(ACT.Sigmoid, I_G, C_HAT, p, t)

        def functions_right(p, t):
            gate_function(ACT.Tanh, C_HAT, B0_G, p, t)
            gate_function(ACT.Sigmoid, B0_G, N_GATES, p, t)

        def gate(p, j):
            return held["gates", p][:, :, j * DH:(j + 1) * DH]

        def rows_of(name, p):
            return held[name, p][:]

        def new_rows(pool, name, p):
            held[name, p] = pool.tile([P, PAIR, DH], F32, name=name)
            return held[name, p][:]

        def mask_of(p, t):
            return m[:, p * PAIR + t:p * PAIR + t + 1]

        def input_product(p, engine):
            if live(p):
                engine.tensor_tensor(
                    out=new_rows(gated_pool, "i_tanh", p), in0=gate(p, I_G), in1=gate(p, C_HAT), op=ALU.mult
                )

        def cell_product(p, engine):
            if live(p):
                c_rows = small_all[:, C_SLOT, p * PAIR:(p + 1) * PAIR, :]
                engine.tensor_tensor(out=new_rows(finish_pool, "f_c", p), in0=gate(p, F_G), in1=c_rows, op=ALU.mult)

        def gates_less_o(p, engine):
            if live(p):
                less_o = finish_pool.tile([P, PAIR, 3, DH], F32, name="less_o")
                gates = held["gates", p][:].rearrange("p t (c d) -> p t c d", c=N_GATES)
                engine.tensor_tensor(
                    out=less_o[:], in0=gates[:, :, B0_G:N_GATES, :],
                    in1=gates[:, :, O_G:O_G + 1, :].to_broadcast([P, PAIR, 3, DH]), op=ALU.subtract,
                )
                for j in range(3):
                    held["g%d" % j, p] = less_o[:, :, j, :]

        def cell_sum(p):
            if live(p):
                nc.vector.tensor_tensor(
                    out=new_rows(finish_pool, "cell", p), in0=held["f_c", p][:], in1=held["i_tanh", p][:], op=ALU.add
                )

        def masked(p, out, name, func):
            for t in range(PAIR):
                nc.scalar.activation(out=out[:, t, :], in_=held[name, p][:, t, :], func=func, scale=mask_of(p, t))

        def cell_tanh(p):
            if live(p):
                masked(p, new_rows(finish_pool, "tanh_c", p), "cell", ACT.Tanh)
                masked(p, new_rows(finish_pool, "tc", p), "tanh_c", ACT.Copy)

        def output_c(p):
            if live(p):
                masked(p, new_rows(out_pool, "c", p), "cell", ACT.Copy)

        def output_h(p):
            if live(p):
                nc.vector.tensor_tensor(out=new_rows(out_pool, "h", p), in0=gate(p, O_G), in1=held["tc", p][:], op=ALU.mult)

        def combine(p, pool, name, in0, scalar, in1, op0, op1):
            if live(p):
                nc.vector.scalar_tensor_tensor(
                    out=new_rows(pool, name, p), in0=rows_of(in0, p), scalar=scalar, in1=rows_of(in1, p), op0=op0, op1=op1
                )

        def output_s0(p):
            combine(p, out_pool, "s0", "g0", 1.0, "tc", ALU.add, ALU.mult)

        def sum_s1(p):
            combine(p, finish_pool, "sum1", "g1", 2.0, "s0", ALU.add, ALU.subtract)

        def part_s2(p):
            combine(p, finish_pool, "part2", "s0", -2.0, "g2", ALU.mult, ALU.add)

        def output_s1(p):
            combine(p, out_pool, "s1", "sum1", 0.5, "tc", ALU.mult, ALU.mult)

        def sum_s2(p):
            combine(p, finish_pool, "sum2", "part2", 3.0, "s1", ALU.add, ALU.subtract)

        def output_s2(p):
            combine(p, out_pool, "s2", "sum2", 1.0 / 3.0, "tc", ALU.mult, ALU.mult)

        def finish_s2(p):
            total = new_rows(finish_pool, "sum2", p)
            s2_out = new_rows(out_pool, "s2", p)
            for t in range(PAIR):
                nc.vector.scalar_tensor_tensor(
                    out=total[:, t, :], in0=rows_of("part2", p)[:, t, :], scalar=3.0, in1=rows_of("s1", p)[:, t, :],
                    op0=ALU.add, op1=ALU.subtract,
                )
            for t in range(PAIR):
                nc.vector.scalar_tensor_tensor(
                    out=s2_out[:, t, :], in0=total[:, t, :], scalar=1.0 / 3.0, in1=rows_of("tc", p)[:, t, :],
                    op0=ALU.mult, op1=ALU.mult,
                )
                row = p * PAIR + t
                nc.sync.dma_start(out=out_rows["s2"][:, row:row + 1, :], in_=s2_out[:, t:t + 1, :])

        def store(p, *names):
            if live(p):
                for name in names:
                    nc.sync.dma_start(out=out_rows[name][:, p * PAIR:(p + 1) * PAIR, :], in_=held[name, p][:])

        nc.scalar.dma_start(out=small_w[:, 0:B0_G, :], in_=weight_hh.rearrange("(c p) d -> p c d", p=P))
        for i, w in enumerate((weight_sh0, weight_sh1, weight_sh2)):
            nc.scalar.dma_start(out=small_w[:, B0_G + i, :], in_=w)
        load_x(0, 0, 1)
        load_x(0, 1, 1)
        nc.scalar.activation(out=warm[:], in_=warm[:], func=ACT.Sigmoid)
        nc.scalar.dma_start(out=bias_rows[0:1, :], in_=bias_ih.rearrange("(r d) -> r d", r=1))
        nc.scalar.dma_start(out=bias_rows[1:2, 0:B0_G * DH], in_=bias_hh.rearrange("(r d) -> r d", r=1))
        for c in range(N_GATES):
            load_weights(c)
        load_small(0, PAIR, range(N_SMALL - 1))
        load_x(0, 2, 1)
        load_x(0, 3, 1)
        load_small(PAIR, X_TILES, range(N_SMALL - 1))
        load_x(1)
        load_small(X_TILES, 2 * X_TILES, range(N_SMALL - 1))
        load_small(0, 2 * X_TILES, range(N_SMALL - 1, N_SMALL))
        for i, b in enumerate((bias_sh0, bias_sh1, bias_sh2)):
            cols = slice((B0_G + i) * DH, (B0_G + i + 1) * DH)
            nc.gpsimd.dma_start(out=bias_rows[1:2, cols], in_=b.rearrange("(r d) -> r d", r=1))
        nc.gpsimd.dma_start(out=mask_bf16[:], in_=mask.rearrange("(p j) -> p j", j=ROWS_PER_PARTITION))
        m = const.tile([P, ROWS_PER_PARTITION], F32, name="m")
        nc.gpsimd.tensor_copy(out=m[:], in_=mask_bf16[:])

        for t in range(PAIR):
            turn_x(0, t)
            copy_x(0, t, s_copy if t == 0 else v_copy)
        quantise_x(0)
        small_wT = const.tile([P, COLS], BF16, name="small_wT")
        for c in range(N_GATES):
            copy_weights(c, v_copy if c in (1, 3) else s_copy)
            if c > 0:
                quantise_weights(c - 1)
            if c == 1:
                small_w_ps = psum_turn.tile([P, N_GATES, P], BF16, name="small_w_ps", tag="turn")
                for i in range(N_GATES):
                    nc.tensor.transpose(small_w_ps[:, i, :], small_w[:, i, :], ident_bf16[:])
                s_copy(out=small_wT[:], in_=small_w_ps[:].rearrange("d c f -> d (c f)"))
        turn_small(0)
        copy_small(0)
        quantise_weights(N_GATES - 1)
        bias_all = const.tile([P, COLS], F32, name="bias_all")
        for cols in (LEFT, RIGHT):
            bias_ps = psum_plain.tile([P, BANK], F32, name="bias_ps", tag="plain")
            width = cols.stop - cols.start
            nc.tensor.matmul(bias_ps[:, 0:width], lhsT=ones[:], rhs=bias_rows[:, cols], start=True, stop=True)
            v_copy(out=bias_all[:, cols], in_=bias_ps[:, 0:width])
        for t in range(PAIR):
            turn_x(1, t)
            copy_x(1, t, s_copy)
        plain(LEFT, 0, 0)
        plain(RIGHT, 0, 0)
        fetch(LEFT, 0, 0)
        fetch(RIGHT, 0, 0)
        mx(RIGHT, 0, 0)
        mx(LEFT, 0, 0)
        turn_small(1)
        copy_small(1)

        for p in range(N_PAIRS):
            if p % 2 == 0:
                load_x(p // 2 + 2)
                load_small((p // 2 + 2) * X_TILES, (p // 2 + 3) * X_TILES)
            if p > 0:
                fetch(LEFT, p, 0)
            plain(RIGHT, p, 1)
            mx(RIGHT, p, 1)
            plain(LEFT, p, 1)
            cell_tanh(p - 2)
            if bias_on_pe(RIGHT, p, 1):
                fetch(RIGHT, p, 1)
            input_product(p - 1, nc.gpsimd)
            gates_less_o(p - 1, nc.gpsimd)
            add_mx(RIGHT, p, 0)
            if not bias_on_pe(RIGHT, p, 1):
                fetch(RIGHT, p, 1)
            functions_right(p, 0)
            output_c(p - 2)
            add_mx(LEFT, p, 0)
            functions_left(p, 0)
            mx(LEFT, p, 1)
            fetch(LEFT, p, 1)
            add_mx(RIGHT, p, 1)
            if p == 0:
                quantise_x(1)
            add_mx(LEFT, p, 1)
            if p < 2:
                plain(RIGHT, p + 1, 0)
            if p < 2:
                fetch(RIGHT, p + 1, 0)
            turn_x(p + 2, 0)
            turn_x(p + 2, 1)
            copy_x(p + 2, 0, s_copy)
            copy_x(p + 2, 1, s_copy)
            if p >= 2:
                plain(RIGHT, p + 1, 0)
            turn_small(p + 2)
            functions_left(p, 1)
            if p >= 2:
                fetch(RIGHT, p + 1, 0)
            functions_right(p, 1)
            copy_small(p + 2)
            output_s0(p - 2)
            cell_product(p - 1, nc.vector)
            sum_s1(p - 2)
            part_s2(p - 2)
            output_s1(p - 2)
            output_h(p - 2)
            sum_s2(p - 2)
            quantise_x(p + 2)
            cell_sum(p - 1)
            output_s2(p - 2)
            plain(LEFT, p + 1, 0)
            mx(RIGHT, p + 1, 0)
            mx(LEFT, p + 1, 0)
            store(p - 2, "c", "h", "s0", "s1", "s2")

        last = N_PAIRS - 1
        cell_tanh(last - 1)
        input_product(last, nc.vector)
        cell_product(last, nc.vector)
        gates_less_o(last, nc.vector)
        cell_sum(last)
        output_c(last - 1)
        store(last - 1, "c")
        cell_tanh(last)
        output_c(last)
        output_s0(last - 1)
        store(last - 1, "s0")
        output_h(last - 1)
        store(last - 1, "h")
        sum_s1(last - 1)
        part_s2(last - 1)
        store(last, "c")
        output_s1(last - 1)
        store(last - 1, "s1")
        output_s0(last)
        store(last, "s0")
        sum_s2(last - 1)
        output_h(last)
        store(last, "h")
        output_s2(last - 1)
        store(last - 1, "s2")
        sum_s1(last)
        part_s2(last)
        output_s1(last)
        store(last, "s1")
        finish_s2(last)
